import numpy as np
import ml_dtypes


def mxq(x, axis, fmt="e4m3"):
    dtype, down = {"e4m3": (ml_dtypes.float8_e4m3fn, 7), "e5m2": (ml_dtypes.float8_e5m2, 14)}[fmt]
    v = np.moveaxis(np.asarray(x, np.float32).astype(ml_dtypes.bfloat16).astype(np.float64), axis, -1)
    blocks = v.reshape(v.shape[:-1] + (-1, 32))
    amax = np.abs(blocks).max(-1, keepdims=True)
    byte = np.maximum(np.where(amax > 0, np.frexp(amax)[1] - 1 + 127, 0) - down, 1)
    scale = np.exp2(byte - 127.0)
    codes = (blocks / scale).astype(np.float32).astype(dtype).astype(np.float64)
    return np.moveaxis((codes * scale).reshape(v.shape), -1, axis)


WIDE = False


def mx_kscale(k):
    if not WIDE:
        return np.ones(k)
    levels = np.array([10, -10, 5, -5, 0])
    if k % 512:
        return np.exp2(np.random.permutation(np.resize(levels, k // 32))).repeat(32)
    a = np.empty((k // 512, 16))
    for p in range(k // 512):
        a[p, :8] = np.random.permutation(np.resize(levels, 8))
        for g in range(8):
            far = levels[np.abs(levels - a[p, g]) >= 10]
            a[p, g + 8] = far[np.random.randint(len(far))]
    return np.exp2(a.ravel()).repeat(32)


BF16 = ml_dtypes.bfloat16


def bf(x):
    return np.asarray(x, np.float32).astype(BF16)


def f64(x):
    return np.asarray(x).astype(np.float64)


B, S, H, D = 2, 128, 16, 128
E = H * D


def rotate_half(u):
    u1, u2 = np.split(u, 2, axis=-1)
    return np.concatenate([-u2, u1], axis=-1)


def draw0():
    s = mx_kscale(E)
    return {"x": bf(np.random.standard_normal((B, S, E)) * s),
            "W": bf(np.random.standard_normal((E, 3 * E)) / np.sqrt(E) / s[:, None]),
            "b": bf(np.random.standard_normal(3 * E) * 0.3)}


def core(x, W, b):
    qkv = (mxq(f64(x), 2, "e4m3") @ mxq(f64(W), 0, "e4m3")) + f64(b)
    qkv = qkv.reshape(B, S, 3, H, D)
    q, k, v = qkv[:, :, 0], qkv[:, :, 1], qkv[:, :, 2]
    t = np.arange(S * D, dtype=np.float64).reshape(1, S, 1, D)
    sin, cos = np.sin(t), np.cos(t)
    q = q * cos + rotate_half(q) * sin
    k = k * cos + rotate_half(k) * sin
    return q, k, v


def e4m3fn_bytes(y):
    return np.clip(np.asarray(y, np.float64), -448.0, 448.0).astype(np.float32).astype(ml_dtypes.float8_e4m3fn).view(np.uint8)


def e4m3fn_values(b):
    return np.asarray(b, np.uint8).view(ml_dtypes.float8_e4m3fn).astype(np.float64)


def setup_inputs():
    d = draw0()
    x0 = np.asarray(d['W']).astype(np.float64)
    s = (np.max(np.abs(x0), axis=(1,), keepdims=True) / 448.0).astype(np.float32)
    out = {}
    for k, v in d.items():
        if k == 'W':
            out['W_bytes'] = e4m3fn_bytes(x0 / s.astype(np.float64))
            out['W_scale'] = s
        else:
            out[k] = v
    return out


def reference(x, W_bytes, W_scale, b):
    return core(x, e4m3fn_values(W_bytes) * W_scale.astype(np.float64), b)

@@ -1,0 +1,316 @@
+import math
+from contextlib import ExitStack
+
+import concourse.mybir as mybir
+from concourse.masks import make_identity
+
+F32 = mybir.dt.float32
+BF16 = mybir.dt.bfloat16
+U32 = mybir.dt.uint32
+U8 = mybir.dt.uint8
+FP8 = mybir.dt.float8_e4m3fn
+FP8X4 = mybir.dt.float8_e4m3fn_x4
+ALU = mybir.AluOpType
+ACT = mybir.ActivationFunctionType
+
+P = 128
+PACK = 4
+K = 2048
+NPASS = 4
+NTOT = 6144
+CW = 1024
+HALF = 512
+NB = NTOT // CW
+NCHUNK = NB * NPASS
+NBATCH = 2
+D = 128
+WBUFS = 8
+
+FLOPS = 2 * 256 * K * NTOT
+
+
+def v_columns(i):
+    if i >= NCHUNK - 1:
+        return 512
+    if i >= 20 or i < 4:
+        return 1024
+    return 768
+
+
+def tile_improvedattention_pa_kernel(tc, x, W_bytes, W_scale, b, out_0, out_1, out_2):
+    nc = tc.nc
+    outs = [o.rearrange("b s h d -> b s (h d)") for o in (out_0, out_1, out_2)]
+    w_rows = W_bytes.rearrange("(g p t) n -> g p t n", p=P, t=PACK)
+
+    with ExitStack() as ctx:
+        const = ctx.enter_context(tc.tile_pool(name="const", bufs=1))
+        wbp = ctx.enter_context(tc.tile_pool(name="wbp", bufs=WBUFS))
+        stage = ctx.enter_context(tc.tile_pool(name="stage", bufs=3))
+        epi = ctx.enter_context(tc.tile_pool(name="epi", bufs=2))
+        psum = ctx.enter_context(tc.psum_pool(name="psum", bufs=8))
+        ctx.enter_context(tc.manual_schedule())
+
+        wb_of = {}
+        planes_of = {}
+        grouped_of = {}
+        codes_of = {}
+        scales_of = {}
+        acc_of = {}
+        work = {}
+
+        def load_chunk(i):
+            nb, g = divmod(i, NPASS)
+            wb = wbp.tile([P, PACK, CW], U8, name="wb", tag="wb")
+            src = w_rows[g][:, :, nb * CW:(nb + 1) * CW]
+            if i == 0:
+                for t in range(PACK):
+                    nc.sync.dma_start(out=wb[:, t, :], in_=src[:, t, :])
+            else:
+                nc.sync.dma_start(out=wb[:], in_=src)
+            wb_of[i] = wb
+
+        wscale = const.tile([P, NPASS * PACK], F32, name="wscale", tag="wscale")
+        nc.scalar.dma_start(
+            out=wscale[:].rearrange("p (g t) -> p g t", t=PACK),
+            in_=W_scale.rearrange("(g p t) o -> p g (t o)", p=P, t=PACK),
+        )
+        load_chunk(0)
+        load_chunk(1)
+        x_sb = []
+        for m in range(NBATCH):
+            xt_sb = const.tile([P, K], BF16, name="x_sb%d" % m, tag="x_sb%d" % m)
+            nc.sync.dma_start(out=xt_sb[:], in_=x[m])
+            x_sb.append(xt_sb)
+        load_chunk(2)
+        load_chunk(3)
+        bias_bc = const.tile([P, NTOT], BF16, name="bias_bc", tag="bias_bc")
+        nc.sync.dma_start(out=bias_bc[:], in_=b.partition_broadcast(P))
+        for i in range(4, WBUFS):
+            load_chunk(i)
+
+        warm_in = const.tile([P, 1], F32, name="warm_in", tag="warm_in")
+        warm_out = const.tile([P, 1], F32, name="warm_out", tag="warm_out")
+        nc.gpsimd.memset(warm_in[:], 0.0)
+        nc.scalar.activation(out=warm_out[:], in_=warm_in[:], func=ACT.Copy)
+        ident = const.tile([P, P], F32, name="ident", tag="ident")
+        make_identity(nc, ident[:])
+
+        def widen(i, ts):
+            g = i % NPASS
+            if i not in planes_of:
+                planes_of[i] = stage.tile([P, PACK, CW], BF16, name="planes", tag="planes")
+            for t in ts:
+                nc.scalar.activation(
+                    out=planes_of[i][:, t, :],
+                    in_=wb_of[i][:, t, :].bitcast(FP8),
+                    func=ACT.Copy,
+                    scale=wscale[:, g * PACK + t:g * PACK + t + 1],
+                )
+
+        widen(0, range(PACK))
+        load_chunk(WBUFS)
+
+        zs = const.tile([P, 3, D], F32, name="zs", tag="zs")
+        zd = const.tile([P, 3, D], F32, name="zd", tag="zd")
+        tmp_s = const.tile([P, 2, D // 2], F32, name="tmp_s", tag="tmp_s")
+        tmp_d = const.tile([P, 2, D // 2], F32, name="tmp_d", tag="tmp_d")
+        chains = ((zs, tmp_s, float(D)), (zd, tmp_d, 1.0))
+        for z, tmp, unit in chains:
+            nc.vector.memset(z[:, :, 0:1], 0.0)
+        for z, tmp, unit in chains:
+            nc.vector.memset(z[:, 1, 0:1], 1.0)
+        for j in range(7):
+            w = 1 << j
+            for z, tmp, unit in chains:
+                nc.vector.tensor_scalar(
+                    out=tmp[:, :, 0:w], in0=z[:, 1:3, 0:w],
+                    scalar1=math.sin(unit * w), scalar2=None, op0=ALU.mult,
+                )
+            for z, tmp, unit in chains:
+                nc.vector.scalar_tensor_tensor(
+                    out=z[:, 0:2, w:2 * w], in0=z[:, 0:2, 0:w], scalar=math.cos(unit * w),
+                    in1=tmp[:, :, 0:w], op0=ALU.mult, op1=ALU.add,
+                )
+            for z, tmp, unit in chains:
+                nc.vector.tensor_scalar(
+                    out=z[:, 2, w:2 * w], in0=z[:, 0, w:2 * w],
+                    scalar1=-1.0, scalar2=None, op0=ALU.mult,
+                )
+
+        xg = []
+        xc = []
+        xs = []
+        x_banks = []
+        for m in range(NBATCH):
+            words = x_sb[m][:].bitcast(F32)
+            for gp in range(NPASS // 2):
+                bank = psum.tile([P, HALF], F32, name="acc", tag="acc")
+                for j in range(4):
+                    g = 2 * gp + j // 2
+                    u = j % 2
+                    nc.tensor.transpose(
+                        bank[:, j * P:(j + 1) * P],
+                        words[:, 256 * g + u:256 * (g + 1):2],
+                        ident[:],
+                    )
+                x_banks.append(bank)
+        tab_t = psum.tile([P, HALF], F32, name="acc", tag="acc")
+        nc.tensor.transpose(tab_t[:, 0:P], zs[:, 0, :], ident[:])
+        nc.tensor.transpose(tab_t[:, P:2 * P], zs[:, 1, :], ident[:])
+
+        def x_prepare():
+            for m in range(NBATCH):
+                g_t = const.tile([P, K], BF16, name="xg%d" % m, tag="xg%d" % m, align_bytes=64)
+                gw = g_t[:].bitcast(F32).rearrange("p (g r u) -> p g r u", g=NPASS, u=2)
+                for gp in range(NPASS // 2):
+                    nc.vector.tensor_copy(
+                        out=gw[:, 2 * gp:2 * gp + 2, :, :],
+                        in_=x_banks[m * 2 + gp][:].rearrange("p (g u r) -> p g r u", g=2, u=2),
+                    )
+                xg.append(g_t)
+            for m in range(NBATCH):
+                c_t = const.tile([P, K // PACK], U32, name="xc%d" % m, tag="xc%d" % m, align_bytes=64)
+                s_t = const.tile([P, K // PACK], U8, name="xs%d" % m, tag="xs%d" % m, align_bytes=64)
+                nc.vector.quantize_mx(out=c_t[:].bitcast(FP8X4), scales=s_t[:], in_=xg[m][:])
+                xc.append(c_t)
+                xs.append(s_t)
+
+        tabs = const.tile([P, 2, CW], F32, name="tabs", tag="tabs")
+        ab = const.tile([P, 2], F32, name="ab", tag="ab")
+        tmp_f = const.tile([P, 2, D], F32, name="tmp_f", tag="tmp_f")
+
+        def tables_a():
+            nc.vector.tensor_copy(out=ab[:], in_=tab_t[:, 0:2 * P:P])
+            nc.vector.tensor_scalar(
+                out=tmp_f[:], in0=zd[:, 1:3, :], scalar1=ab[:, 0:1], scalar2=None, op0=ALU.mult,
+            )
+
+        def tables_b():
+            nc.vector.scalar_tensor_tensor(
+                out=tabs[:, :, 0:D], in0=zd[:, 0:2, :], scalar=ab[:, 1:2],
+                in1=tmp_f[:], op0=ALU.mult, op1=ALU.add,
+            )
+
+        def tables_c():
+            nc.vector.tensor_scalar(
+                out=tabs[:, 0, 0:D // 2], in0=tabs[:, 0, 0:D // 2],
+                scalar1=-1.0, scalar2=None, op0=ALU.mult,
+            )
+
+        def tables_d(w):
+            nc.vector.tensor_copy(out=tabs[:, :, w:2 * w], in_=tabs[:, :, 0:w])
+
+        def interleave(i, engine):
+            cv = v_columns(i)
+            if i not in grouped_of:
+                grouped_of[i] = stage.tile([P, PACK * CW], BF16, name="grouped", tag="grouped", align_bytes=64)
+            dst = grouped_of[i][:].rearrange("p (c t) -> p c t", t=PACK)
+            src = planes_of[i][:].rearrange("p t c -> p c t")
+            if engine == "v":
+                nc.vector.tensor_copy(out=dst[:, 0:cv, :], in_=src[:, 0:cv, :])
+            elif cv < CW:
+                nc.scalar.copy(out=dst[:, cv:CW, :], in_=src[:, cv:CW, :])
+
+        def quantize(i):
+            codes_of[i] = stage.tile([P, CW], U32, name="codes", tag="codes", align_bytes=64)
+            scales_of[i] = stage.tile([P, CW], U8, name="scales", tag="scales", align_bytes=64)
+            nc.vector.quantize_mx(
+                out=codes_of[i][:].bitcast(FP8X4), scales=scales_of[i][:], in_=grouped_of[i][:],
+            )
+
+        def matmuls(i):
+            nb, g = divmod(i, NPASS)
+            if g == 0:
+                for m in range(NBATCH):
+                    for h in range(2):
+                        acc_of[(nb, m, h)] = psum.tile([P, HALF], F32, name="acc", tag="acc")
+            for m in range(NBATCH):
+                for h in range(2):
+                    nc.tensor.matmul_mx(
+                        out=acc_of[(nb, m, h)][:],
+                        lhsT=xc[m][:, g * P:(g + 1) * P].bitcast(FP8X4),
+                        lhsT_scale=xs[m][:, g * P:(g + 1) * P],
+                        rhs=codes_of[i][:, h * HALF:(h + 1) * HALF].bitcast(FP8X4),
+                        rhs_scale=scales_of[i][:, h * HALF:(h + 1) * HALF],
+                        start=(g == 0),
+                        stop=(g == NPASS - 1),
+                    )
+
+        def bias_add(nb, m, h, dst):
+            n0 = nb * CW + h * HALF
+            nc.vector.tensor_tensor(
+                out=dst[:, h * HALF:(h + 1) * HALF], in0=acc_of[(nb, m, h)][:],
+                in1=bias_bc[:, n0:n0 + HALF], op=ALU.add,
+            )
+
+        def store(nb, m, src, c0, c1):
+            col0 = (nb % 2) * CW
+            nc.sync.dma_start(out=outs[nb // 2][m][:, col0 + c0:col0 + c1], in_=src[:, c0:c1])
+
+        def rope_first(nb, m, phase):
+            if phase == 0:
+                work["t"] = epi.tile([P, CW], F32, name="t", tag="t")
+                bias_add(nb, m, 0, work["t"])
+                bias_add(nb, m, 1, work["t"])
+            else:
+                work["r"] = epi.tile([P, CW], F32, name="r", tag="r")
+                t4 = work["t"][:].rearrange("p (h two d) -> p h two d", two=2, d=D // 2)
+                r4 = work["r"][:].rearrange("p (h two d) -> p h two d", two=2, d=D // 2)
+                s4 = tabs[:, 0, :].rearrange("p (h two d) -> p h two d", two=2, d=D // 2)
+                for half in range(2):
+                    nc.vector.tensor_tensor(
+                        out=r4[:, :, half, :], in0=t4[:, :, 1 - half, :], in1=s4[:, :, half, :], op=ALU.mult,
+                    )
+
+        def rope_second(nb, m, phase):
+            if phase == 0:
+                work["a"] = epi.tile([P, CW], F32, name="a", tag="a", bufs=3)
+                nc.vector.tensor_tensor(out=work["a"][:], in0=work["t"][:], in1=tabs[:, 1, :], op=ALU.mult)
+            else:
+                nc.vector.tensor_tensor(out=work["a"][:], in0=work["a"][:], in1=work["r"][:], op=ALU.add)
+                store(nb, m, work["a"], 0, CW)
+
+        for i in range(NCHUNK):
+            nb, g = divmod(i, NPASS)
+            prev = nb - 1
+            if i + 1 < NCHUNK:
+                widen(i + 1, [0])
+            interleave(i, "s")
+            if i + 1 < NCHUNK:
+                widen(i + 1, [1, 2, 3])
+                if i + 1 + WBUFS < NCHUNK:
+                    load_chunk(i + 1 + WBUFS)
+
+            interleave(i, "v")
+            if i == 0:
+                x_prepare()
+            elif i == 1:
+                tables_a()
+            elif i == 2:
+                tables_c()
+            elif i == 3:
+                tables_d(2 * D)
+            elif prev < 4:
+                rope_first(prev, g // 2, g % 2)
+            else:
+                if g % 2 == 0:
+                    work["a"] = epi.tile([P, CW], F32, name="a", tag="a", bufs=3)
+                bias_add(prev, g // 2, g % 2, work["a"])
+            quantize(i)
+            if i == 1:
+                tables_b()
+            elif i == 2:
+                tables_d(D)
+            elif i == 3:
+                tables_d(4 * D)
+            elif i >= 4 and prev < 4:
+                rope_second(prev, g // 2, g % 2)
+            elif i >= 4 and g % 2 == 1:
+                store(prev, g // 2, work["a"], 0, CW)
+            matmuls(i)
+
+        for m in range(NBATCH):
+            work["a"] = epi.tile([P, CW], F32, name="a", tag="a", bufs=3)
+            for h in range(2):
+                bias_add(NB - 1, m, h, work["a"])
+                store(NB - 1, m, work["a"], h * HALF, (h + 1) * HALF)

@@ -17,24 +17,32 @@ P = 128
 PACK = 4
 K = 2048
 NPASS = 4
+NPLANE = NPASS * PACK
 NTOT = 6144
-CW = 1024
-HALF = 512
-NB = NTOT // CW
-NCHUNK = NB * NPASS
+LW = 1024
+UW = 512
+SW = 256
+NLOAD = NTOT // LW
+NUNIT = NTOT // UW
+NSUB = NTOT // SW
+NROPE = 16
 NBATCH = 2
+TOK = 256
 D = 128
-WBUFS = 8
+HD = 64
+WBUFS = 12
+LEAD = 2
 
-FLOPS = 2 * 256 * K * NTOT
+FLOPS = 2 * TOK * K * NTOT
 
-
-def v_columns(i):
-    if i >= NCHUNK - 1:
-        return 512
-    if i >= 20 or i < 4:
-        return 1024
-    return 768
+V_PLANES = {
+    0: [8, 9, 10, 11, 12, 13, 14, 15],
+    1: [13, 14, 15], 2: [13, 14, 15], 3: [13, 14, 15], 4: [13, 14, 15], 5: [13, 14, 15],
+    6: [13, 14, 15], 7: [13, 14, 15], 8: [13, 14, 15], 9: [13, 14, 15],
+    10: [15], 11: [14, 15],
+}
+S_PASSES = {21: 2, 22: 2, 23: 2}
+S2_ON_SCALAR = (0, 1, 2, 3, 4, 5, 6, 7, 8, 9, 10, 11, 12, 13, 14, 15)
 
 
 def tile_improvedattention_pa_kernel(tc, x, W_bytes, W_scale, b, out_0, out_1, out_2):
@@ -46,81 +54,219 @@ def tile_improvedattention_pa_kernel(tc, x, W_bytes, W_scale, b, out_0, out_1, o
         const = ctx.enter_context(tc.tile_pool(name="const", bufs=1))
         wbp = ctx.enter_context(tc.tile_pool(name="wbp", bufs=WBUFS))
         stage = ctx.enter_context(tc.tile_pool(name="stage", bufs=3))
-        epi = ctx.enter_context(tc.tile_pool(name="epi", bufs=2))
-        psum = ctx.enter_context(tc.psum_pool(name="psum", bufs=8))
+        epi = ctx.enter_context(tc.tile_pool(name="epi", bufs=4))
+        psum = ctx.enter_context(tc.psum_pool(name="psum", bufs=4))
         ctx.enter_context(tc.manual_schedule())
 
         wb_of = {}
-        planes_of = {}
+        pl_of = {}
         grouped_of = {}
         codes_of = {}
         scales_of = {}
-        acc_of = {}
-        work = {}
+        mx_of = {}
+        ut_of = {}
+        pq_of = {}
+        e_of = {}
+        o_of = {}
 
-        def load_chunk(i):
-            nb, g = divmod(i, NPASS)
-            wb = wbp.tile([P, PACK, CW], U8, name="wb", tag="wb")
-            src = w_rows[g][:, :, nb * CW:(nb + 1) * CW]
-            if i == 0:
-                for t in range(PACK):
-                    nc.sync.dma_start(out=wb[:, t, :], in_=src[:, t, :])
-            else:
-                nc.sync.dma_start(out=wb[:], in_=src)
-            wb_of[i] = wb
-
-        wscale = const.tile([P, NPASS * PACK], F32, name="wscale", tag="wscale")
+        wscale = const.tile([P, NPLANE], F32, name="wscale", tag="wscale")
         nc.scalar.dma_start(
             out=wscale[:].rearrange("p (g t) -> p g t", t=PACK),
             in_=W_scale.rearrange("(g p t) o -> p g (t o)", p=P, t=PACK),
         )
-        load_chunk(0)
-        load_chunk(1)
+        warm_in = const.tile([P, 1], F32, name="warm_in", tag="warm_in")
+        warm_out = const.tile([P, 1], F32, name="warm_out", tag="warm_out")
+        nc.gpsimd.memset(warm_in[:], 0.0)
+        b_rows = const.tile([P, D], BF16, name="b_rows", tag="b_rows")
+        nc.gpsimd.memset(b_rows[:], 0.0)
+        nc.scalar.dma_start(out=b_rows[0:2 * NROPE, :], in_=b[0:2 * NROPE * D].rearrange("(h d) -> h d", d=D))
+        nc.scalar.activation(out=warm_out[:], in_=warm_in[:], func=ACT.Copy)
+        ident_b = const.tile([P, P], BF16, name="ident_b", tag="ident_b")
+        make_identity(nc, ident_b[:])
+        ident = const.tile([P, P], F32, name="ident", tag="ident")
+        make_identity(nc, ident[:])
+
+        def new_wb(nb, g):
+            wb_of[(nb, g)] = wbp.tile([P, PACK, LW], U8, name="wb", tag="wb")
+
+        def load_cols(nb, g, c0, c1):
+            nc.sync.dma_start(
+                out=wb_of[(nb, g)][:, :, c0:c1], in_=w_rows[g][:, :, nb * LW + c0:nb * LW + c1],
+            )
+
+        for g in range(NPASS):
+            new_wb(0, g)
+        for t in range(PACK):
+            nc.sync.dma_start(out=wb_of[(0, 0)][:, t, 0:UW], in_=w_rows[0][:, t, 0:UW])
+        for g in range(1, NPASS):
+            load_cols(0, g, 0, UW)
         x_sb = []
         for m in range(NBATCH):
             xt_sb = const.tile([P, K], BF16, name="x_sb%d" % m, tag="x_sb%d" % m)
             nc.sync.dma_start(out=xt_sb[:], in_=x[m])
             x_sb.append(xt_sb)
-        load_chunk(2)
-        load_chunk(3)
-        bias_bc = const.tile([P, NTOT], BF16, name="bias_bc", tag="bias_bc")
-        nc.sync.dma_start(out=bias_bc[:], in_=b.partition_broadcast(P))
-        for i in range(4, WBUFS):
-            load_chunk(i)
+        for g in range(NPASS):
+            load_cols(0, g, UW, LW)
+        for g in range(NPASS):
+            new_wb(1, g)
+            load_cols(1, g, 0, LW)
+        bias_v = const.tile([P, K], BF16, name="bias_v", tag="bias_v")
+        nc.sync.dma_start(out=bias_v[:], in_=b[2 * K:3 * K].partition_broadcast(P))
+        for g in range(NPASS):
+            new_wb(2, g)
+            load_cols(2, g, 0, LW)
 
-        warm_in = const.tile([P, 1], F32, name="warm_in", tag="warm_in")
-        warm_out = const.tile([P, 1], F32, name="warm_out", tag="warm_out")
-        nc.gpsimd.memset(warm_in[:], 0.0)
-        nc.scalar.activation(out=warm_out[:], in_=warm_in[:], func=ACT.Copy)
-        ident = const.tile([P, P], F32, name="ident", tag="ident")
-        make_identity(nc, ident[:])
+        def widen(j, gt, on_vector):
+            nb, half = divmod(j, 2)
+            g, t = divmod(gt, PACK)
+            if j not in pl_of:
+                pl_of[j] = stage.tile([P, NPLANE, UW], BF16, name="pl", tag="pl")
+            src = wb_of[(nb, g)][:, t, half * UW:(half + 1) * UW].bitcast(FP8)
+            if on_vector:
+                nc.vector.tensor_scalar(
+                    out=pl_of[j][:, gt, :], in0=src, scalar1=wscale[:, gt:gt + 1], scalar2=None, op0=ALU.mult,
+                )
+            else:
+                nc.scalar.activation(out=pl_of[j][:, gt, :], in_=src, func=ACT.Copy, scale=wscale[:, gt:gt + 1])
 
-        def widen(i, ts):
-            g = i % NPASS
-            if i not in planes_of:
-                planes_of[i] = stage.tile([P, PACK, CW], BF16, name="planes", tag="planes")
-            for t in ts:
-                nc.scalar.activation(
-                    out=planes_of[i][:, t, :],
-                    in_=wb_of[i][:, t, :].bitcast(FP8),
-                    func=ACT.Copy,
-                    scale=wscale[:, g * PACK + t:g * PACK + t + 1],
+        def scalar_planes(q):
+            j, part = divmod(q, 2)
+            if j >= NUNIT:
+                return []
+            mine = [gt for gt in range(part * 8, part * 8 + 8) if gt not in V_PLANES.get(j, [])]
+            return [(j, gt) for gt in mine]
+
+        def interleave(k, on_vector):
+            j, sub = divmod(k, 2)
+            gs = NPASS - S_PASSES.get(k, 0)
+            if k not in grouped_of:
+                grouped_of[k] = stage.tile([P, PACK * NPASS * SW], BF16, name="grouped", tag="grouped", align_bytes=64)
+            dst = grouped_of[k][:].rearrange("p (g c t) -> p g c t", g=NPASS, t=PACK)
+            src = pl_of[j][:].rearrange("p (g t) c -> p g c t", t=PACK)[:, :, sub * SW:(sub + 1) * SW, :]
+            if on_vector:
+                nc.vector.tensor_copy(out=dst[:, 0:gs, :, :], in_=src[:, 0:gs, :, :])
+            else:
+                for g in range(gs, NPASS):
+                    nc.scalar.copy(out=dst[:, g, :, :], in_=src[:, g, :, :])
+
+        def quantize(k):
+            codes_of[k] = stage.tile([P, NPASS * SW], U32, name="codes", tag="codes", align_bytes=64)
+            scales_of[k] = stage.tile([P, NPASS * SW], U8, name="scales", tag="scales", align_bytes=64)
+            nc.vector.quantize_mx(
+                out=codes_of[k][:].bitcast(FP8X4), scales=scales_of[k][:], in_=grouped_of[k][:],
+            )
+
+        xq = {}
+
+        def mx_matmuls(k):
+            mx_of[k] = psum.tile([P, 2 * SW], F32, name="mx", tag="mx")
+            for i in range(2):
+                for g in range(NPASS):
+                    if k < NROPE:
+                        wsl = slice(g * SW + i * D, g * SW + (i + 1) * D)
+                        xsl = slice(g * TOK, (g + 1) * TOK)
+                        lhs_c, lhs_s, rhs_c, rhs_s = codes_of[k], scales_of[k], xq["c"], xq["s"]
+                        lsl, rsl = wsl, xsl
+                    else:
+                        lsl = slice(g * TOK + i * P, g * TOK + (i + 1) * P)
+                        rsl = slice(g * SW, (g + 1) * SW)
+                        lhs_c, lhs_s, rhs_c, rhs_s = xq["c"], xq["s"], codes_of[k], scales_of[k]
+                    nc.tensor.matmul_mx(
+                        out=mx_of[k][:, i * SW:(i + 1) * SW],
+                        lhsT=lhs_c[:, lsl].bitcast(FP8X4),
+                        lhsT_scale=lhs_s[:, lsl],
+                        rhs=rhs_c[:, rsl].bitcast(FP8X4),
+                        rhs_scale=rhs_s[:, rsl],
+                        start=(g == 0),
+                        stop=(g == NPASS - 1),
+                    )
+
+        bias_col = const.tile([P, 2 * NROPE], F32, name="bias_col", tag="bias_col")
+        ab = const.tile([P, 2], F32, name="ab", tag="ab")
+        rot = const.tile([P, 2 * D], F32, name="rot", tag="rot")
+
+        def add_bias_t(k, i):
+            ut_of[(k, i)] = epi.tile([P, TOK], F32, name="ut", tag="ut")
+            head = 2 * k + i
+            nc.scalar.activation(
+                out=ut_of[(k, i)][:], in_=mx_of[k][:, i * TOK:(i + 1) * TOK],
+                func=ACT.Identity, bias=bias_col[:, head:head + 1],
+            )
+
+        def rotate(k, i):
+            pq_of[(k, i)] = psum.tile([P, 2 * TOK], F32, name="pq", tag="pq")
+            for m in range(NBATCH):
+                nc.tensor.matmul(
+                    out=pq_of[(k, i)][:, m * 2 * D:(m + 1) * 2 * D],
+                    lhsT=ut_of[(k, i)][:, m * P:(m + 1) * P],
+                    rhs=rot[:],
+                    start=True,
+                    stop=True,
                 )
 
-        widen(0, range(PACK))
-        load_chunk(WBUFS)
+        def scale_p(k, i):
+            e_of[(k, i)] = epi.tile([P, NBATCH * D], F32, name="e", tag="e")
+            dst = e_of[(k, i)][:].rearrange("p (m d) -> p m d", m=NBATCH)
+            src = pq_of[(k, i)][:].rearrange("p (m z) -> p m z", m=NBATCH)[:, :, 0:D]
+            if k in S2_ON_SCALAR:
+                nc.scalar.activation(out=dst, in_=src, func=ACT.Copy, scale=ab[:, 1:2])
+            else:
+                nc.vector.tensor_scalar(out=dst, in0=src, scalar1=ab[:, 1:2], scalar2=None, op0=ALU.mult)
+
+        def out_tile(k):
+            grp = k // 4
+            if grp not in o_of:
+                o_of[grp] = epi.tile([P, NBATCH, LW], F32, name="o", tag="o", bufs=3)
+            return o_of[grp]
+
+        def store(k, c0, c1):
+            grp = k // 4
+            col0 = (grp % 2) * LW
+            for m in range(NBATCH):
+                nc.sync.dma_start(out=outs[grp // 2][m][:, col0 + c0:col0 + c1], in_=o_of[grp][:, m, c0:c1])
+
+        def combine(k, i):
+            o_t = out_tile(k)
+            off = (k % 4) * SW + i * D
+            nc.vector.scalar_tensor_tensor(
+                out=o_t[:, :, off:off + D],
+                in0=pq_of[(k, i)][:].rearrange("p (m z) -> p m z", m=NBATCH)[:, :, D:2 * D],
+                scalar=ab[:, 0:1],
+                in1=e_of[(k, i)][:].rearrange("p (m d) -> p m d", m=NBATCH),
+                op0=ALU.mult, op1=ALU.add,
+            )
+            if i == 1 and k % 4 == 3:
+                store(k, 0, LW)
+
+        def add_bias_v(k, m):
+            o_t = out_tile(k)
+            off = (k % 4) * SW
+            vcol = (k - NROPE) * SW
+            nc.vector.tensor_tensor(
+                out=o_t[:, m, off:off + SW], in0=mx_of[k][:, m * SW:(m + 1) * SW],
+                in1=bias_v[:, vcol:vcol + SW], op=ALU.add,
+            )
+            if m == 1:
+                if k >= NSUB - 4:
+                    store(k, off, off + SW)
+                elif k % 4 == 3:
+                    store(k, 0, LW)
+
+        for q in range(LEAD):
+            for j, gt in scalar_planes(q):
+                widen(j, gt, False)
 
         zs = const.tile([P, 3, D], F32, name="zs", tag="zs")
         zd = const.tile([P, 3, D], F32, name="zd", tag="zd")
-        tmp_s = const.tile([P, 2, D // 2], F32, name="tmp_s", tag="tmp_s")
-        tmp_d = const.tile([P, 2, D // 2], F32, name="tmp_d", tag="tmp_d")
+        tmp_s = const.tile([P, 2, HD], F32, name="tmp_s", tag="tmp_s")
+        tmp_d = const.tile([P, 2, HD], F32, name="tmp_d", tag="tmp_d")
         chains = ((zs, tmp_s, float(D)), (zd, tmp_d, 1.0))
         for z, tmp, unit in chains:
             nc.vector.memset(z[:, :, 0:1], 0.0)
         for z, tmp, unit in chains:
             nc.vector.memset(z[:, 1, 0:1], 1.0)
-        for j in range(7):
-            w = 1 << j
+        for lev in range(7):
+            w = 1 << lev
             for z, tmp, unit in chains:
                 nc.vector.tensor_scalar(
                     out=tmp[:, :, 0:w], in0=z[:, 1:3, 0:w],
@@ -137,180 +283,130 @@ def tile_improvedattention_pa_kernel(tc, x, W_bytes, W_scale, b, out_0, out_1, o
                     scalar1=-1.0, scalar2=None, op0=ALU.mult,
                 )
 
-        xg = []
-        xc = []
-        xs = []
+        b_t = psum.tile([P, LW], BF16, name="mx", tag="mx")
+        nc.tensor.transpose(b_t[:, 0:P], b_rows[:], ident_b[:])
+        tab_t = psum.tile([P, 2 * SW], F32, name="mx", tag="mx")
+        nc.tensor.transpose(tab_t[:, 0:P], zs[:, 0, :], ident[:])
+        nc.tensor.transpose(tab_t[:, P:2 * P], zs[:, 1, :], ident[:])
         x_banks = []
         for m in range(NBATCH):
             words = x_sb[m][:].bitcast(F32)
             for gp in range(NPASS // 2):
-                bank = psum.tile([P, HALF], F32, name="acc", tag="acc")
-                for j in range(4):
-                    g = 2 * gp + j // 2
-                    u = j % 2
+                bank = psum.tile([P, 2 * SW], F32, name="pq", tag="pq")
+                for i in range(4):
+                    g = 2 * gp + i // 2
+                    u = i % 2
                     nc.tensor.transpose(
-                        bank[:, j * P:(j + 1) * P],
+                        bank[:, i * P:(i + 1) * P],
                         words[:, 256 * g + u:256 * (g + 1):2],
                         ident[:],
                     )
                 x_banks.append(bank)
-        tab_t = psum.tile([P, HALF], F32, name="acc", tag="acc")
-        nc.tensor.transpose(tab_t[:, 0:P], zs[:, 0, :], ident[:])
-        nc.tensor.transpose(tab_t[:, P:2 * P], zs[:, 1, :], ident[:])
+
+        nc.vector.tensor_copy(out=bias_col[:], in_=b_t[:, 0:2 * NROPE])
+        for gt in V_PLANES.get(0, []):
+            widen(0, gt, True)
 
         def x_prepare():
+            xg = const.tile([P, PACK * NPASS * TOK], BF16, name="xg", tag="xg", align_bytes=64)
+            gw = xg[:].bitcast(F32).rearrange("p (g m r u) -> p g m r u", g=NPASS, m=NBATCH, u=2)
             for m in range(NBATCH):
-                g_t = const.tile([P, K], BF16, name="xg%d" % m, tag="xg%d" % m, align_bytes=64)
-                gw = g_t[:].bitcast(F32).rearrange("p (g r u) -> p g r u", g=NPASS, u=2)
                 for gp in range(NPASS // 2):
                     nc.vector.tensor_copy(
-                        out=gw[:, 2 * gp:2 * gp + 2, :, :],
+                        out=gw[:, 2 * gp:2 * gp + 2, m, :, :],
                         in_=x_banks[m * 2 + gp][:].rearrange("p (g u r) -> p g r u", g=2, u=2),
                     )
-                xg.append(g_t)
-            for m in range(NBATCH):
-                c_t = const.tile([P, K // PACK], U32, name="xc%d" % m, tag="xc%d" % m, align_bytes=64)
-                s_t = const.tile([P, K // PACK], U8, name="xs%d" % m, tag="xs%d" % m, align_bytes=64)
-                nc.vector.quantize_mx(out=c_t[:].bitcast(FP8X4), scales=s_t[:], in_=xg[m][:])
-                xc.append(c_t)
-                xs.append(s_t)
+            xq["c"] = const.tile([P, NPASS * TOK], U32, name="xc", tag="xc", align_bytes=64)
+            xq["s"] = const.tile([P, NPASS * TOK], U8, name="xs", tag="xs", align_bytes=64)
+            nc.vector.quantize_mx(out=xq["c"][:].bitcast(FP8X4), scales=xq["s"][:], in_=xg[:])
 
-        tabs = const.tile([P, 2, CW], F32, name="tabs", tag="tabs")
-        ab = const.tile([P, 2], F32, name="ab", tag="ab")
-        tmp_f = const.tile([P, 2, D], F32, name="tmp_f", tag="tmp_f")
+        t_1 = const.tile([P, D], F32, name="t_1", tag="t_1")
+        t_2 = const.tile([P, D], F32, name="t_2", tag="t_2")
 
-        def tables_a():
+        def build_rot_a():
             nc.vector.tensor_copy(out=ab[:], in_=tab_t[:, 0:2 * P:P])
-            nc.vector.tensor_scalar(
-                out=tmp_f[:], in0=zd[:, 1:3, :], scalar1=ab[:, 0:1], scalar2=None, op0=ALU.mult,
-            )
+            nc.vector.tensor_tensor(out=rot[:, 0:D], in0=ident[:], in1=zd[:, 1, :], op=ALU.mult)
+            nc.vector.tensor_tensor(out=t_1[:, 0:HD], in0=ident[:, HD:D], in1=zd[:, 2, 0:HD], op=ALU.mult)
+            nc.vector.tensor_tensor(out=t_1[:, HD:D], in0=ident[:, 0:HD], in1=zd[:, 0, HD:D], op=ALU.mult)
+            nc.vector.tensor_tensor(out=rot[:, D:2 * D], in0=ident[:], in1=zd[:, 2, :], op=ALU.mult)
+            nc.vector.tensor_tensor(out=t_2[:, 0:HD], in0=ident[:, HD:D], in1=zd[:, 1, 0:HD], op=ALU.mult)
+            nc.vector.tensor_tensor(out=t_2[:, HD:D], in0=ident[:, 0:HD], in1=zd[:, 1, HD:D], op=ALU.mult)
 
-        def tables_b():
-            nc.vector.scalar_tensor_tensor(
-                out=tabs[:, :, 0:D], in0=zd[:, 0:2, :], scalar=ab[:, 1:2],
-                in1=tmp_f[:], op0=ALU.mult, op1=ALU.add,
-            )
+        def build_rot_b():
+            nc.vector.tensor_tensor(out=rot[:, 0:D], in0=rot[:, 0:D], in1=t_1[:], op=ALU.add)
+            nc.vector.tensor_tensor(out=rot[:, D:D + HD], in0=rot[:, D:D + HD], in1=t_2[:, 0:HD], op=ALU.subtract)
+            nc.vector.tensor_tensor(out=rot[:, D + HD:2 * D], in0=rot[:, D + HD:2 * D], in1=t_2[:, HD:D], op=ALU.add)
 
-        def tables_c():
-            nc.vector.tensor_scalar(
-                out=tabs[:, 0, 0:D // 2], in0=tabs[:, 0, 0:D // 2],
-                scalar1=-1.0, scalar2=None, op0=ALU.mult,
-            )
+        for k in range(NSUB + 4):
+            if k < NSUB:
+                interleave(k, False)
+            planes = scalar_planes(k + LEAD)
+            rope1 = k - 2
+            rope2 = k - 3
+            for n, (j, gt) in enumerate(planes):
+                if n == 3 and 0 <= rope1 < NROPE:
+                    add_bias_t(rope1, 0)
+                if n == 6 and 0 <= rope1 < NROPE:
+                    add_bias_t(rope1, 1)
+                widen(j, gt, False)
+            if len(planes) <= 6 and 0 <= rope1 < NROPE:
+                if len(planes) <= 3:
+                    add_bias_t(rope1, 0)
+                add_bias_t(rope1, 1)
+            if 0 <= rope2 < NROPE and rope2 in S2_ON_SCALAR:
+                scale_p(rope2, 0)
+                scale_p(rope2, 1)
 
-        def tables_d(w):
-            nc.vector.tensor_copy(out=tabs[:, :, w:2 * w], in_=tabs[:, :, 0:w])
-
-        def interleave(i, engine):
-            cv = v_columns(i)
-            if i not in grouped_of:
-                grouped_of[i] = stage.tile([P, PACK * CW], BF16, name="grouped", tag="grouped", align_bytes=64)
-            dst = grouped_of[i][:].rearrange("p (c t) -> p c t", t=PACK)
-            src = planes_of[i][:].rearrange("p t c -> p c t")
-            if engine == "v":
-                nc.vector.tensor_copy(out=dst[:, 0:cv, :], in_=src[:, 0:cv, :])
-            elif cv < CW:
-                nc.scalar.copy(out=dst[:, cv:CW, :], in_=src[:, cv:CW, :])
-
-        def quantize(i):
-            codes_of[i] = stage.tile([P, CW], U32, name="codes", tag="codes", align_bytes=64)
-            scales_of[i] = stage.tile([P, CW], U8, name="scales", tag="scales", align_bytes=64)
-            nc.vector.quantize_mx(
-                out=codes_of[i][:].bitcast(FP8X4), scales=scales_of[i][:], in_=grouped_of[i][:],
-            )
-
-        def matmuls(i):
-            nb, g = divmod(i, NPASS)
-            if g == 0:
-                for m in range(NBATCH):
-                    for h in range(2):
-                        acc_of[(nb, m, h)] = psum.tile([P, HALF], F32, name="acc", tag="acc")
-            for m in range(NBATCH):
-                for h in range(2):
-                    nc.tensor.matmul_mx(
-                        out=acc_of[(nb, m, h)][:],
-                        lhsT=xc[m][:, g * P:(g + 1) * P].bitcast(FP8X4),
-                        lhsT_scale=xs[m][:, g * P:(g + 1) * P],
-                        rhs=codes_of[i][:, h * HALF:(h + 1) * HALF].bitcast(FP8X4),
-                        rhs_scale=scales_of[i][:, h * HALF:(h + 1) * HALF],
-                        start=(g == 0),
-                        stop=(g == NPASS - 1),
-                    )
-
-        def bias_add(nb, m, h, dst):
-            n0 = nb * CW + h * HALF
-            nc.vector.tensor_tensor(
-                out=dst[:, h * HALF:(h + 1) * HALF], in0=acc_of[(nb, m, h)][:],
-                in1=bias_bc[:, n0:n0 + HALF], op=ALU.add,
-            )
-
-        def store(nb, m, src, c0, c1):
-            col0 = (nb % 2) * CW
-            nc.sync.dma_start(out=outs[nb // 2][m][:, col0 + c0:col0 + c1], in_=src[:, c0:c1])
-
-        def rope_first(nb, m, phase):
-            if phase == 0:
-                work["t"] = epi.tile([P, CW], F32, name="t", tag="t")
-                bias_add(nb, m, 0, work["t"])
-                bias_add(nb, m, 1, work["t"])
-            else:
-                work["r"] = epi.tile([P, CW], F32, name="r", tag="r")
-                t4 = work["t"][:].rearrange("p (h two d) -> p h two d", two=2, d=D // 2)
-                r4 = work["r"][:].rearrange("p (h two d) -> p h two d", two=2, d=D // 2)
-                s4 = tabs[:, 0, :].rearrange("p (h two d) -> p h two d", two=2, d=D // 2)
-                for half in range(2):
-                    nc.vector.tensor_tensor(
-                        out=r4[:, :, half, :], in0=t4[:, :, 1 - half, :], in1=s4[:, :, half, :], op=ALU.mult,
-                    )
-
-        def rope_second(nb, m, phase):
-            if phase == 0:
-                work["a"] = epi.tile([P, CW], F32, name="a", tag="a", bufs=3)
-                nc.vector.tensor_tensor(out=work["a"][:], in0=work["t"][:], in1=tabs[:, 1, :], op=ALU.mult)
-            else:
-                nc.vector.tensor_tensor(out=work["a"][:], in0=work["a"][:], in1=work["r"][:], op=ALU.add)
-                store(nb, m, work["a"], 0, CW)
-
-        for i in range(NCHUNK):
-            nb, g = divmod(i, NPASS)
-            prev = nb - 1
-            if i + 1 < NCHUNK:
-                widen(i + 1, [0])
-            interleave(i, "s")
-            if i + 1 < NCHUNK:
-                widen(i + 1, [1, 2, 3])
-                if i + 1 + WBUFS < NCHUNK:
-                    load_chunk(i + 1 + WBUFS)
-
-            interleave(i, "v")
-            if i == 0:
+            first = []
+            second = []
+            if 0 <= rope2 < NROPE:
+                if rope2 in S2_ON_SCALAR:
+                    first.append(("combine", rope2, 0))
+                    second.append(("combine", rope2, 1))
+                else:
+                    first.append(("scale_p", rope2, 0))
+                    first.append(("scale_p", rope2, 1))
+                    second.append(("combine", rope2, 0))
+                    second.append(("combine", rope2, 1))
+            if NROPE <= k - 1 < NSUB:
+                first.append(("add_bias_v", k - 1, 0))
+                second.append(("add_bias_v", k - 1, 1))
+            ju = (k + 2) // 2
+            if ju >= 1 and (k + 2) % 2 == 0:
+                for gt in V_PLANES.get(ju, []):
+                    first.append(("widen", ju, gt))
+            if k < NSUB:
+                interleave(k, True)
+            if k == 0:
                 x_prepare()
-            elif i == 1:
-                tables_a()
-            elif i == 2:
-                tables_c()
-            elif i == 3:
-                tables_d(2 * D)
-            elif prev < 4:
-                rope_first(prev, g // 2, g % 2)
-            else:
-                if g % 2 == 0:
-                    work["a"] = epi.tile([P, CW], F32, name="a", tag="a", bufs=3)
-                bias_add(prev, g // 2, g % 2, work["a"])
-            quantize(i)
-            if i == 1:
-                tables_b()
-            elif i == 2:
-                tables_d(D)
-            elif i == 3:
-                tables_d(4 * D)
-            elif i >= 4 and prev < 4:
-                rope_second(prev, g // 2, g % 2)
-            elif i >= 4 and g % 2 == 1:
-                store(prev, g // 2, work["a"], 0, CW)
-            matmuls(i)
+            if k == 1:
+                build_rot_b()
+            for what, a0, a1 in first:
+                if what == "scale_p":
+                    scale_p(a0, a1)
+                elif what == "combine":
+                    combine(a0, a1)
+                elif what == "add_bias_v":
+                    add_bias_v(a0, a1)
+                else:
+                    widen(a0, a1, True)
+            if k < NSUB:
+                quantize(k)
+            if k == 0:
+                build_rot_a()
+            for what, a0, a1 in second:
+                if what == "combine":
+                    combine(a0, a1)
+                else:
+                    add_bias_v(a0, a1)
 
-        for m in range(NBATCH):
-            work["a"] = epi.tile([P, CW], F32, name="a", tag="a", bufs=3)
-            for h in range(2):
-                bias_add(NB - 1, m, h, work["a"])
-                store(NB - 1, m, work["a"], h * HALF, (h + 1) * HALF)
+            if k % 4 == 1 and k // 4 + 3 < NLOAD:
+                for g in range(NPASS):
+                    new_wb(k // 4 + 3, g)
+                    load_cols(k // 4 + 3, g, 0, LW)
+
+            if 0 <= rope1 < NROPE:
+                rotate(rope1, 0)
+                rotate(rope1, 1)
+            if k < NSUB:
+                mx_matmuls(k)

@@ -36,13 +36,11 @@ LEAD = 2
 FLOPS = 2 * TOK * K * NTOT
 
 V_PLANES = {
-    0: [8, 9, 10, 11, 12, 13, 14, 15],
-    1: [13, 14, 15], 2: [13, 14, 15], 3: [13, 14, 15], 4: [13, 14, 15], 5: [13, 14, 15],
-    6: [13, 14, 15], 7: [13, 14, 15], 8: [13, 14, 15], 9: [13, 14, 15],
-    10: [15], 11: [14, 15],
+    0: [10, 11, 12, 13, 14, 15],
+    1: [15], 2: [15], 3: [15], 4: [15], 5: [15], 6: [15], 7: [15], 8: [15], 9: [15], 10: [15],
 }
-S_PASSES = {21: 2, 22: 2, 23: 2}
-S2_ON_SCALAR = (0, 1, 2, 3, 4, 5, 6, 7, 8, 9, 10, 11, 12, 13, 14, 15)
+S_PASSES = {22: 2, 23: 2}
+S2_ON_SCALAR = ()
 
 
 def tile_improvedattention_pa_kernel(tc, x, W_bytes, W_scale, b, out_0, out_1, out_2):
@@ -141,13 +139,13 @@ def tile_improvedattention_pa_kernel(tc, x, W_bytes, W_scale, b, out_0, out_1, o
             gs = NPASS - S_PASSES.get(k, 0)
             if k not in grouped_of:
                 grouped_of[k] = stage.tile([P, PACK * NPASS * SW], BF16, name="grouped", tag="grouped", align_bytes=64)
-            dst = grouped_of[k][:].rearrange("p (g c t) -> p g c t", g=NPASS, t=PACK)
-            src = pl_of[j][:].rearrange("p (g t) c -> p g c t", t=PACK)[:, :, sub * SW:(sub + 1) * SW, :]
+            dst = grouped_of[k][:].rearrange("p (g c i t) -> p g c t i", g=NPASS, i=4, t=PACK)
+            src = pl_of[j][:, :, sub * SW:(sub + 1) * SW].rearrange("p (g t) (c i) -> p g c t i", t=PACK, i=4)
             if on_vector:
-                nc.vector.tensor_copy(out=dst[:, 0:gs, :, :], in_=src[:, 0:gs, :, :])
+                nc.vector.tensor_copy(out=dst[:, 0:gs], in_=src[:, 0:gs])
             else:
                 for g in range(gs, NPASS):
-                    nc.scalar.copy(out=dst[:, g, :, :], in_=src[:, g, :, :])
+                    nc.scalar.copy(out=dst[:, g], in_=src[:, g])
 
         def quantize(k):
             codes_of[k] = stage.tile([P, NPASS * SW], U32, name="codes", tag="codes", align_bytes=64)

@@ -37,7 +37,7 @@ FLOPS = 2 * TOK * K * NTOT
 
 V_PLANES = {
     0: [10, 11, 12, 13, 14, 15],
-    1: [15], 2: [15], 3: [15], 4: [15], 5: [15], 6: [15], 7: [15], 8: [15], 9: [15], 10: [15],
+    1: [15], 2: [15], 3: [15], 4: [15], 5: [15],
 }
 S_PASSES = {22: 2, 23: 2}
 S2_ON_SCALAR = ()
@@ -281,6 +281,25 @@ def tile_improvedattention_pa_kernel(tc, x, W_bytes, W_scale, b, out_0, out_1, o
                     scalar1=-1.0, scalar2=None, op0=ALU.mult,
                 )
 
+        t_1 = const.tile([P, D], F32, name="t_1", tag="t_1")
+        t_2 = const.tile([P, D], F32, name="t_2", tag="t_2")
+
+        def build_rot_a():
+            nc.vector.tensor_tensor(out=rot[:, 0:D], in0=ident[:], in1=zd[:, 1, :], op=ALU.mult)
+            nc.vector.tensor_tensor(out=t_1[:, 0:HD], in0=ident[:, HD:D], in1=zd[:, 2, 0:HD], op=ALU.mult)
+            nc.vector.tensor_tensor(out=t_1[:, HD:D], in0=ident[:, 0:HD], in1=zd[:, 0, HD:D], op=ALU.mult)
+            nc.vector.tensor_tensor(out=rot[:, D:2 * D], in0=ident[:], in1=zd[:, 2, :], op=ALU.mult)
+            nc.vector.tensor_tensor(out=t_2[:, 0:HD], in0=ident[:, HD:D], in1=zd[:, 1, 0:HD], op=ALU.mult)
+            nc.vector.tensor_tensor(out=t_2[:, HD:D], in0=ident[:, 0:HD], in1=zd[:, 1, HD:D], op=ALU.mult)
+
+        def build_rot_b():
+            nc.vector.tensor_tensor(out=rot[:, 0:D], in0=rot[:, 0:D], in1=t_1[:], op=ALU.add)
+            nc.vector.tensor_tensor(out=rot[:, D:D + HD], in0=rot[:, D:D + HD], in1=t_2[:, 0:HD], op=ALU.subtract)
+            nc.vector.tensor_tensor(out=rot[:, D + HD:2 * D], in0=rot[:, D + HD:2 * D], in1=t_2[:, HD:D], op=ALU.add)
+
+        build_rot_a()
+        build_rot_b()
+
         b_t = psum.tile([P, LW], BF16, name="mx", tag="mx")
         nc.tensor.transpose(b_t[:, 0:P], b_rows[:], ident_b[:])
         tab_t = psum.tile([P, 2 * SW], F32, name="mx", tag="mx")
@@ -302,6 +321,7 @@ def tile_improvedattention_pa_kernel(tc, x, W_bytes, W_scale, b, out_0, out_1, o
                 x_banks.append(bank)
 
         nc.vector.tensor_copy(out=bias_col[:], in_=b_t[:, 0:2 * NROPE])
+        nc.vector.tensor_copy(out=ab[:], in_=tab_t[:, 0:2 * P:P])
         for gt in V_PLANES.get(0, []):
             widen(0, gt, True)
 
@@ -317,23 +337,6 @@ def tile_improvedattention_pa_kernel(tc, x, W_bytes, W_scale, b, out_0, out_1, o
             xq["c"] = const.tile([P, NPASS * TOK], U32, name="xc", tag="xc", align_bytes=64)
             xq["s"] = const.tile([P, NPASS * TOK], U8, name="xs", tag="xs", align_bytes=64)
             nc.vector.quantize_mx(out=xq["c"][:].bitcast(FP8X4), scales=xq["s"][:], in_=xg[:])
-
-        t_1 = const.tile([P, D], F32, name="t_1", tag="t_1")
-        t_2 = const.tile([P, D], F32, name="t_2", tag="t_2")
-
-        def build_rot_a():
-            nc.vector.tensor_copy(out=ab[:], in_=tab_t[:, 0:2 * P:P])
-            nc.vector.tensor_tensor(out=rot[:, 0:D], in0=ident[:], in1=zd[:, 1, :], op=ALU.mult)
-            nc.vector.tensor_tensor(out=t_1[:, 0:HD], in0=ident[:, HD:D], in1=zd[:, 2, 0:HD], op=ALU.mult)
-            nc.vector.tensor_tensor(out=t_1[:, HD:D], in0=ident[:, 0:HD], in1=zd[:, 0, HD:D], op=ALU.mult)
-            nc.vector.tensor_tensor(out=rot[:, D:2 * D], in0=ident[:], in1=zd[:, 2, :], op=ALU.mult)
-            nc.vector.tensor_tensor(out=t_2[:, 0:HD], in0=ident[:, HD:D], in1=zd[:, 1, 0:HD], op=ALU.mult)
-            nc.vector.tensor_tensor(out=t_2[:, HD:D], in0=ident[:, 0:HD], in1=zd[:, 1, HD:D], op=ALU.mult)
-
-        def build_rot_b():
-            nc.vector.tensor_tensor(out=rot[:, 0:D], in0=rot[:, 0:D], in1=t_1[:], op=ALU.add)
-            nc.vector.tensor_tensor(out=rot[:, D:D + HD], in0=rot[:, D:D + HD], in1=t_2[:, 0:HD], op=ALU.subtract)
-            nc.vector.tensor_tensor(out=rot[:, D + HD:2 * D], in0=rot[:, D + HD:2 * D], in1=t_2[:, HD:D], op=ALU.add)
 
         for k in range(NSUB + 4):
             if k < NSUB:
@@ -377,8 +380,6 @@ def tile_improvedattention_pa_kernel(tc, x, W_bytes, W_scale, b, out_0, out_1, o
                 interleave(k, True)
             if k == 0:
                 x_prepare()
-            if k == 1:
-                build_rot_b()
             for what, a0, a1 in first:
                 if what == "scale_p":
                     scale_p(a0, a1)
@@ -390,8 +391,6 @@ def tile_improvedattention_pa_kernel(tc, x, W_bytes, W_scale, b, out_0, out_1, o
                     widen(a0, a1, True)
             if k < NSUB:
                 quantize(k)
-            if k == 0:
-                build_rot_a()
             for what, a0, a1 in second:
                 if what == "combine":
                     combine(a0, a1)

@@ -16,31 +16,41 @@ ACT = mybir.ActivationFunctionType
 P = 128
 PACK = 4
 K = 2048
-NPASS = 4
-NPLANE = NPASS * PACK
-NTOT = 6144
-LW = 1024
-UW = 512
-SW = 256
-NLOAD = NTOT // LW
-NUNIT = NTOT // UW
-NSUB = NTOT // SW
-NROPE = 16
-NBATCH = 2
-TOK = 256
+PASSES = K // (P * PACK)
+PLANES = PASSES * PACK
+N_ALL = 6144
+BATCH = 2
+TOKENS = BATCH * P
 D = 128
-HD = 64
-WBUFS = 12
+HALF_D = D // 2
+LOAD_COLS = 1024
+UNIT_COLS = 512
+STRIP_COLS = 256
+N_LOADS = N_ALL // LOAD_COLS
+N_UNITS = N_ALL // UNIT_COLS
+N_STRIPS = N_ALL // STRIP_COLS
+ROPE_STRIPS = 2 * K // STRIP_COLS
+ROPE_HEADS = 2 * ROPE_STRIPS
+STRIPS_PER_STORE = LOAD_COLS // STRIP_COLS
+BYTE_TILES = 3 * PASSES
+GROUP = PLANES // 2
 LEAD = 2
 
-FLOPS = 2 * TOK * K * NTOT
+FLOPS = 2 * TOKENS * K * N_ALL
 
-V_PLANES = {
-    0: [10, 11, 12, 13, 14, 15],
-    1: [15], 2: [15], 3: [15], 4: [15], 5: [15],
-}
-S_PASSES = {22: 2, 23: 2}
-S2_ON_SCALAR = ()
+
+def vector_planes(unit):
+    if unit == 0:
+        return list(range(PLANES - 6, PLANES))
+    if unit <= 5:
+        return [PLANES - 2, PLANES - 1]
+    return []
+
+
+def vector_passes(strip):
+    if strip >= N_STRIPS - 2:
+        return PASSES // 2
+    return PASSES
 
 
 def tile_improvedattention_pa_kernel(tc, x, W_bytes, W_scale, b, out_0, out_1, out_2):
@@ -50,26 +60,27 @@ def tile_improvedattention_pa_kernel(tc, x, W_bytes, W_scale, b, out_0, out_1, o
 
     with ExitStack() as ctx:
         const = ctx.enter_context(tc.tile_pool(name="const", bufs=1))
-        wbp = ctx.enter_context(tc.tile_pool(name="wbp", bufs=WBUFS))
+        byte_pool = ctx.enter_context(tc.tile_pool(name="byte_pool", bufs=BYTE_TILES))
         stage = ctx.enter_context(tc.tile_pool(name="stage", bufs=3))
         epi = ctx.enter_context(tc.tile_pool(name="epi", bufs=4))
         psum = ctx.enter_context(tc.psum_pool(name="psum", bufs=4))
         ctx.enter_context(tc.manual_schedule())
 
-        wb_of = {}
-        pl_of = {}
+        w_bytes_of = {}
+        planes_of = {}
         grouped_of = {}
         codes_of = {}
         scales_of = {}
-        mx_of = {}
-        ut_of = {}
+        sums_of = {}
+        u_t_of = {}
         pq_of = {}
-        e_of = {}
-        o_of = {}
+        p_scaled_of = {}
+        out_tile_of = {}
+        x_mx = {}
 
-        wscale = const.tile([P, NPLANE], F32, name="wscale", tag="wscale")
+        w_scale = const.tile([P, PLANES], F32, name="w_scale", tag="w_scale")
         nc.scalar.dma_start(
-            out=wscale[:].rearrange("p (g t) -> p g t", t=PACK),
+            out=w_scale[:].rearrange("p (g t) -> p g t", t=PACK),
             in_=W_scale.rearrange("(g p t) o -> p g (t o)", p=P, t=PACK),
         )
         warm_in = const.tile([P, 1], F32, name="warm_in", tag="warm_in")
@@ -77,333 +88,308 @@ def tile_improvedattention_pa_kernel(tc, x, W_bytes, W_scale, b, out_0, out_1, o
         nc.gpsimd.memset(warm_in[:], 0.0)
         b_rows = const.tile([P, D], BF16, name="b_rows", tag="b_rows")
         nc.gpsimd.memset(b_rows[:], 0.0)
-        nc.scalar.dma_start(out=b_rows[0:2 * NROPE, :], in_=b[0:2 * NROPE * D].rearrange("(h d) -> h d", d=D))
+        nc.scalar.dma_start(out=b_rows[0:ROPE_HEADS, :], in_=b[0:ROPE_HEADS * D].rearrange("(h d) -> h d", d=D))
         nc.scalar.activation(out=warm_out[:], in_=warm_in[:], func=ACT.Copy)
         ident_b = const.tile([P, P], BF16, name="ident_b", tag="ident_b")
         make_identity(nc, ident_b[:])
         ident = const.tile([P, P], F32, name="ident", tag="ident")
         make_identity(nc, ident[:])
 
-        def new_wb(nb, g):
-            wb_of[(nb, g)] = wbp.tile([P, PACK, LW], U8, name="wb", tag="wb")
+        def new_byte_tile(load, g):
+            w_bytes_of[(load, g)] = byte_pool.tile([P, PACK, LOAD_COLS], U8, name="w_bytes", tag="w_bytes")
 
-        def load_cols(nb, g, c0, c1):
+        def load_bytes(load, g, c0, c1):
             nc.sync.dma_start(
-                out=wb_of[(nb, g)][:, :, c0:c1], in_=w_rows[g][:, :, nb * LW + c0:nb * LW + c1],
+                out=w_bytes_of[(load, g)][:, :, c0:c1],
+                in_=w_rows[g][:, :, load * LOAD_COLS + c0:load * LOAD_COLS + c1],
             )
 
-        for g in range(NPASS):
-            new_wb(0, g)
+        for g in range(PASSES):
+            new_byte_tile(0, g)
         for t in range(PACK):
-            nc.sync.dma_start(out=wb_of[(0, 0)][:, t, 0:UW], in_=w_rows[0][:, t, 0:UW])
-        for g in range(1, NPASS):
-            load_cols(0, g, 0, UW)
-        x_sb = []
-        for m in range(NBATCH):
-            xt_sb = const.tile([P, K], BF16, name="x_sb%d" % m, tag="x_sb%d" % m)
-            nc.sync.dma_start(out=xt_sb[:], in_=x[m])
-            x_sb.append(xt_sb)
-        for g in range(NPASS):
-            load_cols(0, g, UW, LW)
-        for g in range(NPASS):
-            new_wb(1, g)
-            load_cols(1, g, 0, LW)
+            nc.sync.dma_start(out=w_bytes_of[(0, 0)][:, t, 0:UNIT_COLS], in_=w_rows[0][:, t, 0:UNIT_COLS])
+        for g in range(1, PASSES):
+            load_bytes(0, g, 0, UNIT_COLS)
+        x_rows = []
+        for m in range(BATCH):
+            x_tile = const.tile([P, K], BF16, name="x_rows%d" % m, tag="x_rows%d" % m)
+            nc.sync.dma_start(out=x_tile[:], in_=x[m])
+            x_rows.append(x_tile)
+        for g in range(PASSES):
+            load_bytes(0, g, UNIT_COLS, LOAD_COLS)
+        for g in range(PASSES):
+            new_byte_tile(1, g)
+            load_bytes(1, g, 0, LOAD_COLS)
         bias_v = const.tile([P, K], BF16, name="bias_v", tag="bias_v")
         nc.sync.dma_start(out=bias_v[:], in_=b[2 * K:3 * K].partition_broadcast(P))
-        for g in range(NPASS):
-            new_wb(2, g)
-            load_cols(2, g, 0, LW)
+        for g in range(PASSES):
+            new_byte_tile(2, g)
+            load_bytes(2, g, 0, LOAD_COLS)
 
-        def widen(j, gt, on_vector):
-            nb, half = divmod(j, 2)
-            g, t = divmod(gt, PACK)
-            if j not in pl_of:
-                pl_of[j] = stage.tile([P, NPLANE, UW], BF16, name="pl", tag="pl")
-            src = wb_of[(nb, g)][:, t, half * UW:(half + 1) * UW].bitcast(FP8)
+        def widen(unit, plane, on_vector):
+            load, half = divmod(unit, LOAD_COLS // UNIT_COLS)
+            g, t = divmod(plane, PACK)
+            if unit not in planes_of:
+                planes_of[unit] = stage.tile([P, PLANES, UNIT_COLS], BF16, name="planes", tag="planes")
+            src = w_bytes_of[(load, g)][:, t, half * UNIT_COLS:(half + 1) * UNIT_COLS].bitcast(FP8)
+            dst = planes_of[unit][:, plane, :]
             if on_vector:
                 nc.vector.tensor_scalar(
-                    out=pl_of[j][:, gt, :], in0=src, scalar1=wscale[:, gt:gt + 1], scalar2=None, op0=ALU.mult,
+                    out=dst, in0=src, scalar1=w_scale[:, plane:plane + 1], scalar2=None, op0=ALU.mult,
                 )
             else:
-                nc.scalar.activation(out=pl_of[j][:, gt, :], in_=src, func=ACT.Copy, scale=wscale[:, gt:gt + 1])
+                nc.scalar.activation(out=dst, in_=src, func=ACT.Copy, scale=w_scale[:, plane:plane + 1])
 
-        def scalar_planes(q):
-            j, part = divmod(q, 2)
-            if j >= NUNIT:
+        def scalar_group(number):
+            unit, part = divmod(number, 2)
+            if unit >= N_UNITS:
                 return []
-            mine = [gt for gt in range(part * 8, part * 8 + 8) if gt not in V_PLANES.get(j, [])]
-            return [(j, gt) for gt in mine]
+            return [
+                (unit, plane) for plane in range(part * GROUP, (part + 1) * GROUP) if plane not in vector_planes(unit)
+            ]
 
-        def interleave(k, on_vector):
-            j, sub = divmod(k, 2)
-            gs = NPASS - S_PASSES.get(k, 0)
-            if k not in grouped_of:
-                grouped_of[k] = stage.tile([P, PACK * NPASS * SW], BF16, name="grouped", tag="grouped", align_bytes=64)
-            dst = grouped_of[k][:].rearrange("p (g c i t) -> p g c t i", g=NPASS, i=4, t=PACK)
-            src = pl_of[j][:, :, sub * SW:(sub + 1) * SW].rearrange("p (g t) (c i) -> p g c t i", t=PACK, i=4)
+        def interleave(strip, on_vector):
+            unit, sub = divmod(strip, UNIT_COLS // STRIP_COLS)
+            if strip not in grouped_of:
+                grouped_of[strip] = stage.tile(
+                    [P, PACK * PASSES * STRIP_COLS], BF16, name="grouped", tag="grouped", align_bytes=64,
+                )
+            dst = grouped_of[strip][:].rearrange("p (g c i t) -> p g c t i", g=PASSES, i=4, t=PACK)
+            src = planes_of[unit][:, :, sub * STRIP_COLS:(sub + 1) * STRIP_COLS].rearrange(
+                "p (g t) (c i) -> p g c t i", t=PACK, i=4,
+            )
+            split = vector_passes(strip)
             if on_vector:
-                nc.vector.tensor_copy(out=dst[:, 0:gs], in_=src[:, 0:gs])
+                nc.vector.tensor_copy(out=dst[:, 0:split], in_=src[:, 0:split])
             else:
-                for g in range(gs, NPASS):
+                for g in range(split, PASSES):
                     nc.scalar.copy(out=dst[:, g], in_=src[:, g])
 
-        def quantize(k):
-            codes_of[k] = stage.tile([P, NPASS * SW], U32, name="codes", tag="codes", align_bytes=64)
-            scales_of[k] = stage.tile([P, NPASS * SW], U8, name="scales", tag="scales", align_bytes=64)
+        def quantize(strip):
+            codes_of[strip] = stage.tile([P, PASSES * STRIP_COLS], U32, name="codes", tag="codes", align_bytes=64)
+            scales_of[strip] = stage.tile([P, PASSES * STRIP_COLS], U8, name="scales", tag="scales", align_bytes=64)
             nc.vector.quantize_mx(
-                out=codes_of[k][:].bitcast(FP8X4), scales=scales_of[k][:], in_=grouped_of[k][:],
+                out=codes_of[strip][:].bitcast(FP8X4), scales=scales_of[strip][:], in_=grouped_of[strip][:],
             )
 
-        xq = {}
-
-        def mx_matmuls(k):
-            mx_of[k] = psum.tile([P, 2 * SW], F32, name="mx", tag="mx")
+        def mx_matmuls(strip):
+            sums_of[strip] = psum.tile([P, 2 * STRIP_COLS], F32, name="mx", tag="mx")
+            w_c, w_s = codes_of[strip], scales_of[strip]
             for i in range(2):
-                for g in range(NPASS):
-                    if k < NROPE:
-                        wsl = slice(g * SW + i * D, g * SW + (i + 1) * D)
-                        xsl = slice(g * TOK, (g + 1) * TOK)
-                        lhs_c, lhs_s, rhs_c, rhs_s = codes_of[k], scales_of[k], xq["c"], xq["s"]
-                        lsl, rsl = wsl, xsl
+                for g in range(PASSES):
+                    if strip < ROPE_STRIPS:
+                        lhs_c, lhs_s, lhs_cols = w_c, w_s, slice(g * STRIP_COLS + i * D, g * STRIP_COLS + (i + 1) * D)
+                        rhs_c, rhs_s, rhs_cols = x_mx["codes"], x_mx["scales"], slice(g * TOKENS, (g + 1) * TOKENS)
                     else:
-                        lsl = slice(g * TOK + i * P, g * TOK + (i + 1) * P)
-                        rsl = slice(g * SW, (g + 1) * SW)
-                        lhs_c, lhs_s, rhs_c, rhs_s = xq["c"], xq["s"], codes_of[k], scales_of[k]
+                        lhs_c, lhs_s, lhs_cols = x_mx["codes"], x_mx["scales"], slice(g * TOKENS + i * P, g * TOKENS + (i + 1) * P)
+                        rhs_c, rhs_s, rhs_cols = w_c, w_s, slice(g * STRIP_COLS, (g + 1) * STRIP_COLS)
                     nc.tensor.matmul_mx(
-                        out=mx_of[k][:, i * SW:(i + 1) * SW],
-                        lhsT=lhs_c[:, lsl].bitcast(FP8X4),
-                        lhsT_scale=lhs_s[:, lsl],
-                        rhs=rhs_c[:, rsl].bitcast(FP8X4),
-                        rhs_scale=rhs_s[:, rsl],
+                        out=sums_of[strip][:, i * STRIP_COLS:(i + 1) * STRIP_COLS],
+                        lhsT=lhs_c[:, lhs_cols].bitcast(FP8X4),
+                        lhsT_scale=lhs_s[:, lhs_cols],
+                        rhs=rhs_c[:, rhs_cols].bitcast(FP8X4),
+                        rhs_scale=rhs_s[:, rhs_cols],
                         start=(g == 0),
-                        stop=(g == NPASS - 1),
+                        stop=(g == PASSES - 1),
                     )
 
-        bias_col = const.tile([P, 2 * NROPE], F32, name="bias_col", tag="bias_col")
-        ab = const.tile([P, 2], F32, name="ab", tag="ab")
-        rot = const.tile([P, 2 * D], F32, name="rot", tag="rot")
+        bias_col = const.tile([P, ROPE_HEADS], F32, name="bias_col", tag="bias_col")
+        sin_cos_s = const.tile([P, 2], F32, name="sin_cos_s", tag="sin_cos_s")
+        r1_r2 = const.tile([P, 2 * D], F32, name="r1_r2", tag="r1_r2")
 
-        def add_bias_t(k, i):
-            ut_of[(k, i)] = epi.tile([P, TOK], F32, name="ut", tag="ut")
-            head = 2 * k + i
+        def add_bias_transposed(strip, i):
+            u_t_of[(strip, i)] = epi.tile([P, TOKENS], F32, name="u_t", tag="u_t")
+            head = 2 * strip + i
             nc.scalar.activation(
-                out=ut_of[(k, i)][:], in_=mx_of[k][:, i * TOK:(i + 1) * TOK],
+                out=u_t_of[(strip, i)][:], in_=sums_of[strip][:, i * TOKENS:(i + 1) * TOKENS],
                 func=ACT.Identity, bias=bias_col[:, head:head + 1],
             )
 
-        def rotate(k, i):
-            pq_of[(k, i)] = psum.tile([P, 2 * TOK], F32, name="pq", tag="pq")
-            for m in range(NBATCH):
+        def rotate_by_d(strip, i):
+            pq_of[(strip, i)] = psum.tile([P, BATCH * 2 * D], F32, name="pq", tag="pq")
+            for m in range(BATCH):
                 nc.tensor.matmul(
-                    out=pq_of[(k, i)][:, m * 2 * D:(m + 1) * 2 * D],
-                    lhsT=ut_of[(k, i)][:, m * P:(m + 1) * P],
-                    rhs=rot[:],
+                    out=pq_of[(strip, i)][:, m * 2 * D:(m + 1) * 2 * D],
+                    lhsT=u_t_of[(strip, i)][:, m * P:(m + 1) * P],
+                    rhs=r1_r2[:],
                     start=True,
                     stop=True,
                 )
 
-        def scale_p(k, i):
-            e_of[(k, i)] = epi.tile([P, NBATCH * D], F32, name="e", tag="e")
-            dst = e_of[(k, i)][:].rearrange("p (m d) -> p m d", m=NBATCH)
-            src = pq_of[(k, i)][:].rearrange("p (m z) -> p m z", m=NBATCH)[:, :, 0:D]
-            if k in S2_ON_SCALAR:
-                nc.scalar.activation(out=dst, in_=src, func=ACT.Copy, scale=ab[:, 1:2])
-            else:
-                nc.vector.tensor_scalar(out=dst, in0=src, scalar1=ab[:, 1:2], scalar2=None, op0=ALU.mult)
+        def scale_p(strip, i):
+            p_scaled_of[(strip, i)] = epi.tile([P, BATCH * D], F32, name="p_scaled", tag="p_scaled")
+            nc.vector.tensor_scalar(
+                out=p_scaled_of[(strip, i)][:].rearrange("p (m d) -> p m d", m=BATCH),
+                in0=pq_of[(strip, i)][:].rearrange("p (m z) -> p m z", m=BATCH)[:, :, 0:D],
+                scalar1=sin_cos_s[:, 1:2], scalar2=None, op0=ALU.mult,
+            )
 
-        def out_tile(k):
-            grp = k // 4
-            if grp not in o_of:
-                o_of[grp] = epi.tile([P, NBATCH, LW], F32, name="o", tag="o", bufs=3)
-            return o_of[grp]
+        def out_tile(strip):
+            number = strip // STRIPS_PER_STORE
+            if number not in out_tile_of:
+                out_tile_of[number] = epi.tile([P, BATCH, LOAD_COLS], F32, name="out_tile", tag="out_tile", bufs=3)
+            return out_tile_of[number]
 
-        def store(k, c0, c1):
-            grp = k // 4
-            col0 = (grp % 2) * LW
-            for m in range(NBATCH):
-                nc.sync.dma_start(out=outs[grp // 2][m][:, col0 + c0:col0 + c1], in_=o_of[grp][:, m, c0:c1])
+        def store(strip, c0, c1):
+            number = strip // STRIPS_PER_STORE
+            first_col = (number % 2) * LOAD_COLS
+            for m in range(BATCH):
+                nc.sync.dma_start(
+                    out=outs[number // 2][m][:, first_col + c0:first_col + c1], in_=out_tile_of[number][:, m, c0:c1],
+                )
 
-        def combine(k, i):
-            o_t = out_tile(k)
-            off = (k % 4) * SW + i * D
+        def add_scaled_q(strip, i):
+            first_col = (strip % STRIPS_PER_STORE) * STRIP_COLS + i * D
             nc.vector.scalar_tensor_tensor(
-                out=o_t[:, :, off:off + D],
-                in0=pq_of[(k, i)][:].rearrange("p (m z) -> p m z", m=NBATCH)[:, :, D:2 * D],
-                scalar=ab[:, 0:1],
-                in1=e_of[(k, i)][:].rearrange("p (m d) -> p m d", m=NBATCH),
+                out=out_tile(strip)[:, :, first_col:first_col + D],
+                in0=pq_of[(strip, i)][:].rearrange("p (m z) -> p m z", m=BATCH)[:, :, D:2 * D],
+                scalar=sin_cos_s[:, 0:1],
+                in1=p_scaled_of[(strip, i)][:].rearrange("p (m d) -> p m d", m=BATCH),
                 op0=ALU.mult, op1=ALU.add,
             )
-            if i == 1 and k % 4 == 3:
-                store(k, 0, LW)
+            if i == 1 and strip % STRIPS_PER_STORE == STRIPS_PER_STORE - 1:
+                store(strip, 0, LOAD_COLS)
 
-        def add_bias_v(k, m):
-            o_t = out_tile(k)
-            off = (k % 4) * SW
-            vcol = (k - NROPE) * SW
+        def add_bias_v(strip, m):
+            first_col = (strip % STRIPS_PER_STORE) * STRIP_COLS
+            v_col = (strip - ROPE_STRIPS) * STRIP_COLS
             nc.vector.tensor_tensor(
-                out=o_t[:, m, off:off + SW], in0=mx_of[k][:, m * SW:(m + 1) * SW],
-                in1=bias_v[:, vcol:vcol + SW], op=ALU.add,
+                out=out_tile(strip)[:, m, first_col:first_col + STRIP_COLS],
+                in0=sums_of[strip][:, m * STRIP_COLS:(m + 1) * STRIP_COLS],
+                in1=bias_v[:, v_col:v_col + STRIP_COLS], op=ALU.add,
             )
-            if m == 1:
-                if k >= NSUB - 4:
-                    store(k, off, off + SW)
-                elif k % 4 == 3:
-                    store(k, 0, LW)
+            if m == BATCH - 1:
+                if strip >= N_STRIPS - STRIPS_PER_STORE:
+                    store(strip, first_col, first_col + STRIP_COLS)
+                elif strip % STRIPS_PER_STORE == STRIPS_PER_STORE - 1:
+                    store(strip, 0, LOAD_COLS)
 
-        for q in range(LEAD):
-            for j, gt in scalar_planes(q):
-                widen(j, gt, False)
+        for number in range(LEAD):
+            for unit, plane in scalar_group(number):
+                widen(unit, plane, False)
 
-        zs = const.tile([P, 3, D], F32, name="zs", tag="zs")
-        zd = const.tile([P, 3, D], F32, name="zd", tag="zd")
-        tmp_s = const.tile([P, 2, HD], F32, name="tmp_s", tag="tmp_s")
-        tmp_d = const.tile([P, 2, HD], F32, name="tmp_d", tag="tmp_d")
-        chains = ((zs, tmp_s, float(D)), (zd, tmp_d, 1.0))
-        for z, tmp, unit in chains:
-            nc.vector.memset(z[:, :, 0:1], 0.0)
-        for z, tmp, unit in chains:
-            nc.vector.memset(z[:, 1, 0:1], 1.0)
-        for lev in range(7):
-            w = 1 << lev
-            for z, tmp, unit in chains:
+        table_s = const.tile([P, 3, D], F32, name="table_s", tag="table_s")
+        table_d = const.tile([P, 3, D], F32, name="table_d", tag="table_d")
+        cross_s = const.tile([P, 2, HALF_D], F32, name="cross_s", tag="cross_s")
+        cross_d = const.tile([P, 2, HALF_D], F32, name="cross_d", tag="cross_d")
+        tables = ((table_s, cross_s, float(D)), (table_d, cross_d, 1.0))
+        for table, cross, step in tables:
+            nc.vector.memset(table[:, :, 0:1], 0.0)
+        for table, cross, step in tables:
+            nc.vector.memset(table[:, 1, 0:1], 1.0)
+        for level in range(7):
+            w = 1 << level
+            for table, cross, step in tables:
                 nc.vector.tensor_scalar(
-                    out=tmp[:, :, 0:w], in0=z[:, 1:3, 0:w],
-                    scalar1=math.sin(unit * w), scalar2=None, op0=ALU.mult,
+                    out=cross[:, :, 0:w], in0=table[:, 1:3, 0:w],
+                    scalar1=math.sin(step * w), scalar2=None, op0=ALU.mult,
                 )
-            for z, tmp, unit in chains:
+            for table, cross, step in tables:
                 nc.vector.scalar_tensor_tensor(
-                    out=z[:, 0:2, w:2 * w], in0=z[:, 0:2, 0:w], scalar=math.cos(unit * w),
-                    in1=tmp[:, :, 0:w], op0=ALU.mult, op1=ALU.add,
+                    out=table[:, 0:2, w:2 * w], in0=table[:, 0:2, 0:w], scalar=math.cos(step * w),
+                    in1=cross[:, :, 0:w], op0=ALU.mult, op1=ALU.add,
                 )
-            for z, tmp, unit in chains:
+            for table, cross, step in tables:
                 nc.vector.tensor_scalar(
-                    out=z[:, 2, w:2 * w], in0=z[:, 0, w:2 * w],
+                    out=table[:, 2, w:2 * w], in0=table[:, 0, w:2 * w],
                     scalar1=-1.0, scalar2=None, op0=ALU.mult,
                 )
 
-        t_1 = const.tile([P, D], F32, name="t_1", tag="t_1")
-        t_2 = const.tile([P, D], F32, name="t_2", tag="t_2")
+        sin_d, cos_d, neg_sin_d = table_d[:, 0, :], table_d[:, 1, :], table_d[:, 2, :]
+        lo, hi = slice(0, HALF_D), slice(HALF_D, D)
+        off_1 = const.tile([P, D], F32, name="off_1", tag="off_1")
+        off_2 = const.tile([P, D], F32, name="off_2", tag="off_2")
+        nc.vector.tensor_tensor(out=r1_r2[:, 0:D], in0=ident[:], in1=cos_d, op=ALU.mult)
+        nc.vector.tensor_tensor(out=off_1[:, lo], in0=ident[:, hi], in1=neg_sin_d[:, lo], op=ALU.mult)
+        nc.vector.tensor_tensor(out=off_1[:, hi], in0=ident[:, lo], in1=sin_d[:, hi], op=ALU.mult)
+        nc.vector.tensor_tensor(out=r1_r2[:, D:2 * D], in0=ident[:], in1=neg_sin_d, op=ALU.mult)
+        nc.vector.tensor_tensor(out=off_2[:, lo], in0=ident[:, hi], in1=cos_d[:, lo], op=ALU.mult)
+        nc.vector.tensor_tensor(out=off_2[:, hi], in0=ident[:, lo], in1=cos_d[:, hi], op=ALU.mult)
+        nc.vector.tensor_tensor(out=r1_r2[:, 0:D], in0=r1_r2[:, 0:D], in1=off_1[:], op=ALU.add)
+        nc.vector.tensor_tensor(
+            out=r1_r2[:, D:D + HALF_D], in0=r1_r2[:, D:D + HALF_D], in1=off_2[:, lo], op=ALU.subtract,
+        )
+        nc.vector.tensor_tensor(
+            out=r1_r2[:, D + HALF_D:2 * D], in0=r1_r2[:, D + HALF_D:2 * D], in1=off_2[:, hi], op=ALU.add,
+        )
 
-        def build_rot_a():
-            nc.vector.tensor_tensor(out=rot[:, 0:D], in0=ident[:], in1=zd[:, 1, :], op=ALU.mult)
-            nc.vector.tensor_tensor(out=t_1[:, 0:HD], in0=ident[:, HD:D], in1=zd[:, 2, 0:HD], op=ALU.mult)
-            nc.vector.tensor_tensor(out=t_1[:, HD:D], in0=ident[:, 0:HD], in1=zd[:, 0, HD:D], op=ALU.mult)
-            nc.vector.tensor_tensor(out=rot[:, D:2 * D], in0=ident[:], in1=zd[:, 2, :], op=ALU.mult)
-            nc.vector.tensor_tensor(out=t_2[:, 0:HD], in0=ident[:, HD:D], in1=zd[:, 1, 0:HD], op=ALU.mult)
-            nc.vector.tensor_tensor(out=t_2[:, HD:D], in0=ident[:, 0:HD], in1=zd[:, 1, HD:D], op=ALU.mult)
-
-        def build_rot_b():
-            nc.vector.tensor_tensor(out=rot[:, 0:D], in0=rot[:, 0:D], in1=t_1[:], op=ALU.add)
-            nc.vector.tensor_tensor(out=rot[:, D:D + HD], in0=rot[:, D:D + HD], in1=t_2[:, 0:HD], op=ALU.subtract)
-            nc.vector.tensor_tensor(out=rot[:, D + HD:2 * D], in0=rot[:, D + HD:2 * D], in1=t_2[:, HD:D], op=ALU.add)
-
-        build_rot_a()
-        build_rot_b()
-
-        b_t = psum.tile([P, LW], BF16, name="mx", tag="mx")
-        nc.tensor.transpose(b_t[:, 0:P], b_rows[:], ident_b[:])
-        tab_t = psum.tile([P, 2 * SW], F32, name="mx", tag="mx")
-        nc.tensor.transpose(tab_t[:, 0:P], zs[:, 0, :], ident[:])
-        nc.tensor.transpose(tab_t[:, P:2 * P], zs[:, 1, :], ident[:])
+        b_turned = psum.tile([P, 2 * 2 * STRIP_COLS], BF16, name="mx", tag="mx")
+        nc.tensor.transpose(b_turned[:, 0:P], b_rows[:], ident_b[:])
+        s_turned = psum.tile([P, 2 * STRIP_COLS], F32, name="mx", tag="mx")
+        nc.tensor.transpose(s_turned[:, 0:P], table_s[:, 0, :], ident[:])
+        nc.tensor.transpose(s_turned[:, P:2 * P], table_s[:, 1, :], ident[:])
         x_banks = []
-        for m in range(NBATCH):
-            words = x_sb[m][:].bitcast(F32)
-            for gp in range(NPASS // 2):
-                bank = psum.tile([P, 2 * SW], F32, name="pq", tag="pq")
+        for m in range(BATCH):
+            words = x_rows[m][:].bitcast(F32)
+            for pair in range(PASSES // 2):
+                bank = psum.tile([P, 2 * STRIP_COLS], F32, name="pq", tag="pq")
                 for i in range(4):
-                    g = 2 * gp + i // 2
+                    g = 2 * pair + i // 2
                     u = i % 2
-                    nc.tensor.transpose(
-                        bank[:, i * P:(i + 1) * P],
-                        words[:, 256 * g + u:256 * (g + 1):2],
-                        ident[:],
-                    )
+                    nc.tensor.transpose(bank[:, i * P:(i + 1) * P], words[:, 256 * g + u:256 * (g + 1):2], ident[:])
                 x_banks.append(bank)
 
-        nc.vector.tensor_copy(out=bias_col[:], in_=b_t[:, 0:2 * NROPE])
-        nc.vector.tensor_copy(out=ab[:], in_=tab_t[:, 0:2 * P:P])
-        for gt in V_PLANES.get(0, []):
-            widen(0, gt, True)
+        nc.vector.tensor_copy(out=bias_col[:], in_=b_turned[:, 0:ROPE_HEADS])
+        nc.vector.tensor_copy(out=sin_cos_s[:], in_=s_turned[:, 0:2 * P:P])
+        for plane in vector_planes(0):
+            widen(0, plane, True)
 
-        def x_prepare():
-            xg = const.tile([P, PACK * NPASS * TOK], BF16, name="xg", tag="xg", align_bytes=64)
-            gw = xg[:].bitcast(F32).rearrange("p (g m r u) -> p g m r u", g=NPASS, m=NBATCH, u=2)
-            for m in range(NBATCH):
-                for gp in range(NPASS // 2):
+        def quantize_x():
+            x_grouped = const.tile([P, PACK * PASSES * TOKENS], BF16, name="x_grouped", tag="x_grouped", align_bytes=64)
+            as_words = x_grouped[:].bitcast(F32).rearrange("p (g m r u) -> p g m r u", g=PASSES, m=BATCH, u=2)
+            for m in range(BATCH):
+                for pair in range(PASSES // 2):
                     nc.vector.tensor_copy(
-                        out=gw[:, 2 * gp:2 * gp + 2, m, :, :],
-                        in_=x_banks[m * 2 + gp][:].rearrange("p (g u r) -> p g r u", g=2, u=2),
+                        out=as_words[:, 2 * pair:2 * pair + 2, m, :, :],
+                        in_=x_banks[m * 2 + pair][:].rearrange("p (g u r) -> p g r u", g=2, u=2),
                     )
-            xq["c"] = const.tile([P, NPASS * TOK], U32, name="xc", tag="xc", align_bytes=64)
-            xq["s"] = const.tile([P, NPASS * TOK], U8, name="xs", tag="xs", align_bytes=64)
-            nc.vector.quantize_mx(out=xq["c"][:].bitcast(FP8X4), scales=xq["s"][:], in_=xg[:])
+            x_mx["codes"] = const.tile([P, PASSES * TOKENS], U32, name="x_codes", tag="x_codes", align_bytes=64)
+            x_mx["scales"] = const.tile([P, PASSES * TOKENS], U8, name="x_scales", tag="x_scales", align_bytes=64)
+            nc.vector.quantize_mx(out=x_mx["codes"][:].bitcast(FP8X4), scales=x_mx["scales"][:], in_=x_grouped[:])
 
-        for k in range(NSUB + 4):
-            if k < NSUB:
+        for k in range(N_STRIPS + 1):
+            biased = k - 2
+            scaled = k - 3
+            v_done = k - 1
+
+            if k < N_STRIPS:
                 interleave(k, False)
-            planes = scalar_planes(k + LEAD)
-            rope1 = k - 2
-            rope2 = k - 3
-            for n, (j, gt) in enumerate(planes):
-                if n == 3 and 0 <= rope1 < NROPE:
-                    add_bias_t(rope1, 0)
-                if n == 6 and 0 <= rope1 < NROPE:
-                    add_bias_t(rope1, 1)
-                widen(j, gt, False)
-            if len(planes) <= 6 and 0 <= rope1 < NROPE:
-                if len(planes) <= 3:
-                    add_bias_t(rope1, 0)
-                add_bias_t(rope1, 1)
-            if 0 <= rope2 < NROPE and rope2 in S2_ON_SCALAR:
-                scale_p(rope2, 0)
-                scale_p(rope2, 1)
+            group = scalar_group(k + LEAD)
+            for unit, plane in group[0:GROUP // 2]:
+                widen(unit, plane, False)
+            if 0 <= biased < ROPE_STRIPS:
+                add_bias_transposed(biased, 0)
+                add_bias_transposed(biased, 1)
+            for unit, plane in group[GROUP // 2:]:
+                widen(unit, plane, False)
 
-            first = []
-            second = []
-            if 0 <= rope2 < NROPE:
-                if rope2 in S2_ON_SCALAR:
-                    first.append(("combine", rope2, 0))
-                    second.append(("combine", rope2, 1))
-                else:
-                    first.append(("scale_p", rope2, 0))
-                    first.append(("scale_p", rope2, 1))
-                    second.append(("combine", rope2, 0))
-                    second.append(("combine", rope2, 1))
-            if NROPE <= k - 1 < NSUB:
-                first.append(("add_bias_v", k - 1, 0))
-                second.append(("add_bias_v", k - 1, 1))
-            ju = (k + 2) // 2
-            if ju >= 1 and (k + 2) % 2 == 0:
-                for gt in V_PLANES.get(ju, []):
-                    first.append(("widen", ju, gt))
-            if k < NSUB:
+            if k < N_STRIPS:
                 interleave(k, True)
             if k == 0:
-                x_prepare()
-            for what, a0, a1 in first:
-                if what == "scale_p":
-                    scale_p(a0, a1)
-                elif what == "combine":
-                    combine(a0, a1)
-                elif what == "add_bias_v":
-                    add_bias_v(a0, a1)
-                else:
-                    widen(a0, a1, True)
-            if k < NSUB:
+                quantize_x()
+            if 0 <= scaled < ROPE_STRIPS:
+                scale_p(scaled, 0)
+                scale_p(scaled, 1)
+            if ROPE_STRIPS <= v_done:
+                add_bias_v(v_done, 0)
+            if k % 2 == 0:
+                for plane in vector_planes(k // 2 + 1):
+                    widen(k // 2 + 1, plane, True)
+            if k < N_STRIPS:
                 quantize(k)
-            for what, a0, a1 in second:
-                if what == "combine":
-                    combine(a0, a1)
-                else:
-                    add_bias_v(a0, a1)
+            if 0 <= scaled < ROPE_STRIPS:
+                add_scaled_q(scaled, 0)
+                add_scaled_q(scaled, 1)
+            if ROPE_STRIPS <= v_done:
+                add_bias_v(v_done, 1)
 
-            if k % 4 == 1 and k // 4 + 3 < NLOAD:
-                for g in range(NPASS):
-                    new_wb(k // 4 + 3, g)
-                    load_cols(k // 4 + 3, g, 0, LW)
+            if k % 4 == 1 and k // 4 + 3 < N_LOADS:
+                for g in range(PASSES):
+                    new_byte_tile(k // 4 + 3, g)
+                    load_bytes(k // 4 + 3, g, 0, LOAD_COLS)
 
-            if 0 <= rope1 < NROPE:
-                rotate(rope1, 0)
-                rotate(rope1, 1)
-            if k < NSUB:
+            if 0 <= biased < ROPE_STRIPS:
+                rotate_by_d(biased, 0)
+                rotate_by_d(biased, 1)
+            if k < N_STRIPS:
                 mx_matmuls(k)

@@ -34,7 +34,10 @@ ROPE_HEADS = 2 * ROPE_STRIPS
 STRIPS_PER_STORE = LOAD_COLS // STRIP_COLS
 BYTE_TILES = 3 * PASSES
 GROUP = PLANES // 2
-LEAD = 2
+LEAD = 3
+LAST_PLANE = PLANES - 1
+LAST_PASS = PASSES - 1
+GPSIMD_STRIPS = range(3, 19)
 
 FLOPS = 2 * TOKENS * K * N_ALL
 
@@ -42,14 +45,28 @@ FLOPS = 2 * TOKENS * K * N_ALL
 def vector_planes(unit):
     if unit == 0:
         return list(range(PLANES - 6, PLANES))
-    if unit <= 5:
-        return [PLANES - 2, PLANES - 1]
     return []
+
+
+def scalar_columns(unit, plane):
+    if plane in vector_planes(unit):
+        return None
+    c0, c1 = 0, UNIT_COLS
+    if plane == LAST_PLANE:
+        if 2 * unit in GPSIMD_STRIPS:
+            c0 = STRIP_COLS
+        if 2 * unit + 1 in GPSIMD_STRIPS:
+            c1 = STRIP_COLS
+    if c0 >= c1:
+        return None
+    return (c0, c1)
 
 
 def vector_passes(strip):
     if strip >= N_STRIPS - 2:
         return PASSES // 2
+    if strip >= GPSIMD_STRIPS.start:
+        return PASSES - 1
     return PASSES
 
 
@@ -126,13 +143,13 @@ def tile_improvedattention_pa_kernel(tc, x, W_bytes, W_scale, b, out_0, out_1, o
             new_byte_tile(2, g)
             load_bytes(2, g, 0, LOAD_COLS)
 
-        def widen(unit, plane, on_vector):
+        def widen(unit, plane, on_vector, c0=0, c1=UNIT_COLS):
             load, half = divmod(unit, LOAD_COLS // UNIT_COLS)
             g, t = divmod(plane, PACK)
             if unit not in planes_of:
                 planes_of[unit] = stage.tile([P, PLANES, UNIT_COLS], BF16, name="planes", tag="planes")
-            src = w_bytes_of[(load, g)][:, t, half * UNIT_COLS:(half + 1) * UNIT_COLS].bitcast(FP8)
-            dst = planes_of[unit][:, plane, :]
+            src = w_bytes_of[(load, g)][:, t, half * UNIT_COLS + c0:half * UNIT_COLS + c1].bitcast(FP8)
+            dst = planes_of[unit][:, plane, c0:c1]
             if on_vector:
                 nc.vector.tensor_scalar(
                     out=dst, in0=src, scalar1=w_scale[:, plane:plane + 1], scalar2=None, op0=ALU.mult,
@@ -145,10 +162,14 @@ def tile_improvedattention_pa_kernel(tc, x, W_bytes, W_scale, b, out_0, out_1, o
             if unit >= N_UNITS:
                 return []
             return [
-                (unit, plane) for plane in range(part * GROUP, (part + 1) * GROUP) if plane not in vector_planes(unit)
+                (unit, plane) for plane in range(part * GROUP, (part + 1) * GROUP) if scalar_columns(unit, plane)
             ]
 
-        def interleave(strip, on_vector):
+        def scalar_widen(unit, plane):
+            c0, c1 = scalar_columns(unit, plane)
+            widen(unit, plane, False, c0, c1)
+
+        def interleave(strip, engine):
             unit, sub = divmod(strip, UNIT_COLS // STRIP_COLS)
             if strip not in grouped_of:
                 grouped_of[strip] = stage.tile(
@@ -159,11 +180,24 @@ def tile_improvedattention_pa_kernel(tc, x, W_bytes, W_scale, b, out_0, out_1, o
                 "p (g t) (c i) -> p g c t i", t=PACK, i=4,
             )
             split = vector_passes(strip)
-            if on_vector:
-                nc.vector.tensor_copy(out=dst[:, 0:split], in_=src[:, 0:split])
+            if engine == "vector, first part":
+                first = split - split % 2
+                nc.vector.tensor_copy(out=dst[:, 0:first], in_=src[:, 0:first])
+            elif engine == "vector, second part":
+                if split % 2:
+                    nc.vector.tensor_copy(out=dst[:, split - 1], in_=src[:, split - 1])
+            elif engine == "scalar":
+                if strip not in GPSIMD_STRIPS:
+                    for g in range(split, PASSES):
+                        nc.scalar.copy(out=dst[:, g], in_=src[:, g])
             else:
-                for g in range(split, PASSES):
-                    nc.scalar.copy(out=dst[:, g], in_=src[:, g])
+                nc.gpsimd.tensor_scalar(
+                    out=grouped_of[strip][:].rearrange("p (g c t) -> p g c t", g=PASSES, t=PACK)[:, LAST_PASS],
+                    in0=planes_of[unit][:, :, sub * STRIP_COLS:(sub + 1) * STRIP_COLS].rearrange(
+                        "p (g t) c -> p g c t", t=PACK,
+                    )[:, LAST_PASS],
+                    scalar1=1.0, scalar2=0.0, op0=ALU.mult, op1=ALU.add,
+                )
 
         def quantize(strip):
             codes_of[strip] = stage.tile([P, PASSES * STRIP_COLS], U32, name="codes", tag="codes", align_bytes=64)
@@ -200,9 +234,9 @@ def tile_improvedattention_pa_kernel(tc, x, W_bytes, W_scale, b, out_0, out_1, o
         def add_bias_transposed(strip, i):
             u_t_of[(strip, i)] = epi.tile([P, TOKENS], F32, name="u_t", tag="u_t")
             head = 2 * strip + i
-            nc.scalar.activation(
-                out=u_t_of[(strip, i)][:], in_=sums_of[strip][:, i * TOKENS:(i + 1) * TOKENS],
-                func=ACT.Identity, bias=bias_col[:, head:head + 1],
+            nc.vector.tensor_scalar(
+                out=u_t_of[(strip, i)][:], in0=sums_of[strip][:, i * TOKENS:(i + 1) * TOKENS],
+                scalar1=bias_col[:, head:head + 1], scalar2=None, op0=ALU.add,
             )
 
         def rotate_by_d(strip, i):
@@ -266,7 +300,7 @@ def tile_improvedattention_pa_kernel(tc, x, W_bytes, W_scale, b, out_0, out_1, o
 
         for number in range(LEAD):
             for unit, plane in scalar_group(number):
-                widen(unit, plane, False)
+                scalar_widen(unit, plane)
 
         table_s = const.tile([P, 3, D], F32, name="table_s", tag="table_s")
         table_d = const.tile([P, 3, D], F32, name="table_d", tag="table_d")
@@ -348,42 +382,40 @@ def tile_improvedattention_pa_kernel(tc, x, W_bytes, W_scale, b, out_0, out_1, o
             nc.vector.quantize_mx(out=x_mx["codes"][:].bitcast(FP8X4), scales=x_mx["scales"][:], in_=x_grouped[:])
 
         for k in range(N_STRIPS + 1):
-            biased = k - 2
-            scaled = k - 3
+            biased = k - 1
+            scaled = k - 2
             v_done = k - 1
 
             if k < N_STRIPS:
-                interleave(k, False)
-            group = scalar_group(k + LEAD)
-            for unit, plane in group[0:GROUP // 2]:
-                widen(unit, plane, False)
+                interleave(k, "scalar")
+            for unit, plane in scalar_group(k + LEAD):
+                scalar_widen(unit, plane)
+
+            if k < N_STRIPS:
+                interleave(k, "vector, first part")
+            if k + 1 in GPSIMD_STRIPS:
+                unit, sub = divmod(k + 1, UNIT_COLS // STRIP_COLS)
+                widen(unit, LAST_PLANE, True, sub * STRIP_COLS, (sub + 1) * STRIP_COLS)
+                interleave(k + 1, "gpsimd")
+            if k < N_STRIPS:
+                interleave(k, "vector, second part")
+            if k == 0:
+                quantize_x()
             if 0 <= biased < ROPE_STRIPS:
                 add_bias_transposed(biased, 0)
                 add_bias_transposed(biased, 1)
-            for unit, plane in group[GROUP // 2:]:
-                widen(unit, plane, False)
-
-            if k < N_STRIPS:
-                interleave(k, True)
-            if k == 0:
-                quantize_x()
             if 0 <= scaled < ROPE_STRIPS:
                 scale_p(scaled, 0)
                 scale_p(scaled, 1)
-            if ROPE_STRIPS <= v_done:
-                add_bias_v(v_done, 0)
-            if k % 2 == 0:
-                for plane in vector_planes(k // 2 + 1):
-                    widen(k // 2 + 1, plane, True)
-            if k < N_STRIPS:
-                quantize(k)
-            if 0 <= scaled < ROPE_STRIPS:
                 add_scaled_q(scaled, 0)
                 add_scaled_q(scaled, 1)
             if ROPE_STRIPS <= v_done:
+                add_bias_v(v_done, 0)
                 add_bias_v(v_done, 1)
+            if k < N_STRIPS:
+                quantize(k)
 
-            if k % 4 == 1 and k // 4 + 3 < N_LOADS:
+            if k % 4 == 2 and k // 4 + 3 < N_LOADS:
                 for g in range(PASSES):
                     new_byte_tile(k // 4 + 3, g)
                     load_bytes(k // 4 + 3, g, 0, LOAD_COLS)

@@ -35,9 +35,6 @@ STRIPS_PER_STORE = LOAD_COLS // STRIP_COLS
 BYTE_TILES = 3 * PASSES
 GROUP = PLANES // 2
 LEAD = 3
-LAST_PLANE = PLANES - 1
-LAST_PASS = PASSES - 1
-GPSIMD_STRIPS = range(3, 19)
 
 FLOPS = 2 * TOKENS * K * N_ALL
 
@@ -48,26 +45,18 @@ def vector_planes(unit):
     return []
 
 
-def scalar_columns(unit, plane):
-    if plane in vector_planes(unit):
-        return None
-    c0, c1 = 0, UNIT_COLS
-    if plane == LAST_PLANE:
-        if 2 * unit in GPSIMD_STRIPS:
-            c0 = STRIP_COLS
-        if 2 * unit + 1 in GPSIMD_STRIPS:
-            c1 = STRIP_COLS
-    if c0 >= c1:
-        return None
-    return (c0, c1)
+def gpsimd_columns(strip):
+    if 4 <= strip <= 19:
+        return 64
+    return 0
 
 
-def vector_passes(strip):
+def scalar_columns(strip):
     if strip >= N_STRIPS - 2:
-        return PASSES // 2
-    if strip >= GPSIMD_STRIPS.start:
-        return PASSES - 1
-    return PASSES
+        return 128
+    if strip > 19:
+        return 64
+    return 0
 
 
 def tile_improvedattention_pa_kernel(tc, x, W_bytes, W_scale, b, out_0, out_1, out_2):
@@ -143,13 +132,13 @@ def tile_improvedattention_pa_kernel(tc, x, W_bytes, W_scale, b, out_0, out_1, o
             new_byte_tile(2, g)
             load_bytes(2, g, 0, LOAD_COLS)
 
-        def widen(unit, plane, on_vector, c0=0, c1=UNIT_COLS):
+        def widen(unit, plane, on_vector):
             load, half = divmod(unit, LOAD_COLS // UNIT_COLS)
             g, t = divmod(plane, PACK)
             if unit not in planes_of:
                 planes_of[unit] = stage.tile([P, PLANES, UNIT_COLS], BF16, name="planes", tag="planes")
-            src = w_bytes_of[(load, g)][:, t, half * UNIT_COLS + c0:half * UNIT_COLS + c1].bitcast(FP8)
-            dst = planes_of[unit][:, plane, c0:c1]
+            src = w_bytes_of[(load, g)][:, t, half * UNIT_COLS:(half + 1) * UNIT_COLS].bitcast(FP8)
+            dst = planes_of[unit][:, plane, :]
             if on_vector:
                 nc.vector.tensor_scalar(
                     out=dst, in0=src, scalar1=w_scale[:, plane:plane + 1], scalar2=None, op0=ALU.mult,
@@ -162,40 +151,32 @@ def tile_improvedattention_pa_kernel(tc, x, W_bytes, W_scale, b, out_0, out_1, o
             if unit >= N_UNITS:
                 return []
             return [
-                (unit, plane) for plane in range(part * GROUP, (part + 1) * GROUP) if scalar_columns(unit, plane)
+                (unit, plane) for plane in range(part * GROUP, (part + 1) * GROUP) if plane not in vector_planes(unit)
             ]
-
-        def scalar_widen(unit, plane):
-            c0, c1 = scalar_columns(unit, plane)
-            widen(unit, plane, False, c0, c1)
 
         def interleave(strip, engine):
             unit, sub = divmod(strip, UNIT_COLS // STRIP_COLS)
             if strip not in grouped_of:
                 grouped_of[strip] = stage.tile(
-                    [P, PACK * PASSES * STRIP_COLS], BF16, name="grouped", tag="grouped", align_bytes=64,
+                    [P, PACK * PASSES * STRIP_COLS], BF16, name="grouped", tag="grouped", align_bytes=64, bufs=2,
                 )
-            dst = grouped_of[strip][:].rearrange("p (g c i t) -> p g c t i", g=PASSES, i=4, t=PACK)
-            src = planes_of[unit][:, :, sub * STRIP_COLS:(sub + 1) * STRIP_COLS].rearrange(
-                "p (g t) (c i) -> p g c t i", t=PACK, i=4,
-            )
-            split = vector_passes(strip)
-            if engine == "vector, first part":
-                first = split - split % 2
-                nc.vector.tensor_copy(out=dst[:, 0:first], in_=src[:, 0:first])
-            elif engine == "vector, second part":
-                if split % 2:
-                    nc.vector.tensor_copy(out=dst[:, split - 1], in_=src[:, split - 1])
+            split = STRIP_COLS - gpsimd_columns(strip) - scalar_columns(strip)
+            dst = grouped_of[strip][:].rearrange("p (g c t) -> p g c t", g=PASSES, t=PACK)
+            src = planes_of[unit][:, :, sub * STRIP_COLS:(sub + 1) * STRIP_COLS].rearrange("p (g t) c -> p g c t", t=PACK)
+            if engine == "vector":
+                nc.vector.tensor_copy(
+                    out=dst[:, :, 0:split, :].rearrange("p g (c i) t -> p g c t i", i=4),
+                    in_=src[:, :, 0:split, :].rearrange("p g (c i) t -> p g c t i", i=4),
+                )
             elif engine == "scalar":
-                if strip not in GPSIMD_STRIPS:
-                    for g in range(split, PASSES):
-                        nc.scalar.copy(out=dst[:, g], in_=src[:, g])
-            else:
+                if scalar_columns(strip):
+                    nc.scalar.copy(
+                        out=dst[:, :, split:STRIP_COLS, :].rearrange("p g (c i) t -> p g c t i", i=4),
+                        in_=src[:, :, split:STRIP_COLS, :].rearrange("p g (c i) t -> p g c t i", i=4),
+                    )
+            elif gpsimd_columns(strip):
                 nc.gpsimd.tensor_scalar(
-                    out=grouped_of[strip][:].rearrange("p (g c t) -> p g c t", g=PASSES, t=PACK)[:, LAST_PASS],
-                    in0=planes_of[unit][:, :, sub * STRIP_COLS:(sub + 1) * STRIP_COLS].rearrange(
-                        "p (g t) c -> p g c t", t=PACK,
-                    )[:, LAST_PASS],
+                    out=dst[:, :, split:STRIP_COLS, :], in0=src[:, :, split:STRIP_COLS, :],
                     scalar1=1.0, scalar2=0.0, op0=ALU.mult, op1=ALU.add,
                 )
 
@@ -231,30 +212,33 @@ def tile_improvedattention_pa_kernel(tc, x, W_bytes, W_scale, b, out_0, out_1, o
         sin_cos_s = const.tile([P, 2], F32, name="sin_cos_s", tag="sin_cos_s")
         r1_r2 = const.tile([P, 2 * D], F32, name="r1_r2", tag="r1_r2")
 
-        def add_bias_transposed(strip, i):
-            u_t_of[(strip, i)] = epi.tile([P, TOKENS], F32, name="u_t", tag="u_t")
-            head = 2 * strip + i
-            nc.vector.tensor_scalar(
-                out=u_t_of[(strip, i)][:], in0=sums_of[strip][:, i * TOKENS:(i + 1) * TOKENS],
-                scalar1=bias_col[:, head:head + 1], scalar2=None, op0=ALU.add,
+        def add_bias_transposed(strip):
+            u_t_of[strip] = epi.tile([P, 2 * TOKENS], F32, name="u_t", tag="u_t")
+            nc.vector.tensor_tensor(
+                out=u_t_of[strip][:].rearrange("p (i n) -> p i n", i=2),
+                in0=sums_of[strip][:].rearrange("p (i n) -> p i n", i=2),
+                in1=bias_col[:, 2 * strip:2 * strip + 2].unsqueeze(2).to_broadcast([P, 2, TOKENS]),
+                op=ALU.add,
             )
 
-        def rotate_by_d(strip, i):
-            pq_of[(strip, i)] = psum.tile([P, BATCH * 2 * D], F32, name="pq", tag="pq")
-            for m in range(BATCH):
-                nc.tensor.matmul(
-                    out=pq_of[(strip, i)][:, m * 2 * D:(m + 1) * 2 * D],
-                    lhsT=u_t_of[(strip, i)][:, m * P:(m + 1) * P],
-                    rhs=r1_r2[:],
-                    start=True,
-                    stop=True,
-                )
+        def rotate_by_d(strip):
+            pq_of[(strip, 0)] = psum.tile([P, 2 * STRIP_COLS], F32, name="pq", tag="pq")
+            pq_of[(strip, 1)] = psum.tile([P, 2 * STRIP_COLS], F32, name="pq", tag="pq")
+            for i in range(2):
+                for m in range(BATCH):
+                    for z in range(2):
+                        nc.tensor.matmul(
+                            out=pq_of[(strip, z)][:, m * STRIP_COLS + i * D:m * STRIP_COLS + (i + 1) * D],
+                            lhsT=u_t_of[strip][:, i * TOKENS + m * P:i * TOKENS + (m + 1) * P],
+                            rhs=r1_r2[:, z * D:(z + 1) * D],
+                            start=True,
+                            stop=True,
+                        )
 
-        def scale_p(strip, i):
-            p_scaled_of[(strip, i)] = epi.tile([P, BATCH * D], F32, name="p_scaled", tag="p_scaled")
+        def scale_p(strip):
+            p_scaled_of[strip] = epi.tile([P, 2 * STRIP_COLS], F32, name="p_scaled", tag="p_scaled")
             nc.vector.tensor_scalar(
-                out=p_scaled_of[(strip, i)][:].rearrange("p (m d) -> p m d", m=BATCH),
-                in0=pq_of[(strip, i)][:].rearrange("p (m z) -> p m z", m=BATCH)[:, :, 0:D],
+                out=p_scaled_of[strip][:], in0=pq_of[(strip, 0)][:],
                 scalar1=sin_cos_s[:, 1:2], scalar2=None, op0=ALU.mult,
             )
 
@@ -272,35 +256,35 @@ def tile_improvedattention_pa_kernel(tc, x, W_bytes, W_scale, b, out_0, out_1, o
                     out=outs[number // 2][m][:, first_col + c0:first_col + c1], in_=out_tile_of[number][:, m, c0:c1],
                 )
 
-        def add_scaled_q(strip, i):
-            first_col = (strip % STRIPS_PER_STORE) * STRIP_COLS + i * D
+        def add_scaled_q(strip):
+            first_col = (strip % STRIPS_PER_STORE) * STRIP_COLS
             nc.vector.scalar_tensor_tensor(
-                out=out_tile(strip)[:, :, first_col:first_col + D],
-                in0=pq_of[(strip, i)][:].rearrange("p (m z) -> p m z", m=BATCH)[:, :, D:2 * D],
+                out=out_tile(strip)[:, :, first_col:first_col + STRIP_COLS],
+                in0=pq_of[(strip, 1)][:].rearrange("p (m z) -> p m z", m=BATCH),
                 scalar=sin_cos_s[:, 0:1],
-                in1=p_scaled_of[(strip, i)][:].rearrange("p (m d) -> p m d", m=BATCH),
+                in1=p_scaled_of[strip][:].rearrange("p (m z) -> p m z", m=BATCH),
                 op0=ALU.mult, op1=ALU.add,
             )
-            if i == 1 and strip % STRIPS_PER_STORE == STRIPS_PER_STORE - 1:
+            if strip % STRIPS_PER_STORE == STRIPS_PER_STORE - 1:
                 store(strip, 0, LOAD_COLS)
 
-        def add_bias_v(strip, m):
+        def add_bias_v(strip):
             first_col = (strip % STRIPS_PER_STORE) * STRIP_COLS
             v_col = (strip - ROPE_STRIPS) * STRIP_COLS
             nc.vector.tensor_tensor(
-                out=out_tile(strip)[:, m, first_col:first_col + STRIP_COLS],
-                in0=sums_of[strip][:, m * STRIP_COLS:(m + 1) * STRIP_COLS],
-                in1=bias_v[:, v_col:v_col + STRIP_COLS], op=ALU.add,
+                out=out_tile(strip)[:, :, first_col:first_col + STRIP_COLS],
+                in0=sums_of[strip][:].rearrange("p (m c) -> p m c", m=BATCH),
+                in1=bias_v[:, v_col:v_col + STRIP_COLS].unsqueeze(1).to_broadcast([P, BATCH, STRIP_COLS]),
+                op=ALU.add,
             )
-            if m == BATCH - 1:
-                if strip >= N_STRIPS - STRIPS_PER_STORE:
-                    store(strip, first_col, first_col + STRIP_COLS)
-                elif strip % STRIPS_PER_STORE == STRIPS_PER_STORE - 1:
-                    store(strip, 0, LOAD_COLS)
+            if strip >= N_STRIPS - STRIPS_PER_STORE:
+                store(strip, first_col, first_col + STRIP_COLS)
+            elif strip % STRIPS_PER_STORE == STRIPS_PER_STORE - 1:
+                store(strip, 0, LOAD_COLS)
 
         for number in range(LEAD):
             for unit, plane in scalar_group(number):
-                scalar_widen(unit, plane)
+                widen(unit, plane, False)
 
         table_s = const.tile([P, 3, D], F32, name="table_s", tag="table_s")
         table_d = const.tile([P, 3, D], F32, name="table_d", tag="table_d")
@@ -381,47 +365,43 @@ def tile_improvedattention_pa_kernel(tc, x, W_bytes, W_scale, b, out_0, out_1, o
             x_mx["scales"] = const.tile([P, PASSES * TOKENS], U8, name="x_scales", tag="x_scales", align_bytes=64)
             nc.vector.quantize_mx(out=x_mx["codes"][:].bitcast(FP8X4), scales=x_mx["scales"][:], in_=x_grouped[:])
 
-        for k in range(N_STRIPS + 1):
-            biased = k - 1
-            scaled = k - 2
-            v_done = k - 1
+        for k in range(N_STRIPS + 2):
+            biased = k - 2
+            scaled = k - 3
+            v_done = k - 2
 
             if k < N_STRIPS:
                 interleave(k, "scalar")
             for unit, plane in scalar_group(k + LEAD):
-                scalar_widen(unit, plane)
+                widen(unit, plane, False)
+
+            if k + 1 < N_STRIPS:
+                interleave(k + 1, "gpsimd")
 
             if k < N_STRIPS:
-                interleave(k, "vector, first part")
-            if k + 1 in GPSIMD_STRIPS:
-                unit, sub = divmod(k + 1, UNIT_COLS // STRIP_COLS)
-                widen(unit, LAST_PLANE, True, sub * STRIP_COLS, (sub + 1) * STRIP_COLS)
-                interleave(k + 1, "gpsimd")
-            if k < N_STRIPS:
-                interleave(k, "vector, second part")
+                interleave(k, "vector")
             if k == 0:
                 quantize_x()
-            if 0 <= biased < ROPE_STRIPS:
-                add_bias_transposed(biased, 0)
-                add_bias_transposed(biased, 1)
             if 0 <= scaled < ROPE_STRIPS:
-                scale_p(scaled, 0)
-                scale_p(scaled, 1)
-                add_scaled_q(scaled, 0)
-                add_scaled_q(scaled, 1)
-            if ROPE_STRIPS <= v_done:
-                add_bias_v(v_done, 0)
-                add_bias_v(v_done, 1)
+                scale_p(scaled)
+            if 0 <= biased < ROPE_STRIPS:
+                add_bias_transposed(biased)
+            if 0 <= scaled < ROPE_STRIPS:
+                add_scaled_q(scaled)
+            if ROPE_STRIPS <= v_done < N_STRIPS:
+                add_bias_v(v_done)
+            if k % 2 == 0 and k // 2 + 1 < N_UNITS:
+                for plane in vector_planes(k // 2 + 1):
+                    widen(k // 2 + 1, plane, True)
             if k < N_STRIPS:
                 quantize(k)
 
-            if k % 4 == 2 and k // 4 + 3 < N_LOADS:
+            if k % 4 == 0 and k // 4 + 3 < N_LOADS:
                 for g in range(PASSES):
                     new_byte_tile(k // 4 + 3, g)
                     load_bytes(k // 4 + 3, g, 0, LOAD_COLS)
 
             if 0 <= biased < ROPE_STRIPS:
-                rotate_by_d(biased, 0)
-                rotate_by_d(biased, 1)
+                rotate_by_d(biased)
             if k < N_STRIPS:
                 mx_matmuls(k)

@@ -34,6 +34,8 @@ ROPE_HEADS = 2 * ROPE_STRIPS
 STRIPS_PER_STORE = LOAD_COLS // STRIP_COLS
 BYTE_TILES = 3 * PASSES
 GROUP = PLANES // 2
+DOUBLINGS = 7
+TABLE_ROWS = 4
 LEAD = 3
 
 FLOPS = 2 * TOKENS * K * N_ALL
@@ -41,7 +43,7 @@ FLOPS = 2 * TOKENS * K * N_ALL
 
 def vector_planes(unit):
     if unit == 0:
-        return list(range(PLANES - 6, PLANES))
+        return list(range(PLANES - 10, PLANES))
     return []
 
 
@@ -116,12 +118,14 @@ def tile_improvedattention_pa_kernel(tc, x, W_bytes, W_scale, b, out_0, out_1, o
             nc.sync.dma_start(out=w_bytes_of[(0, 0)][:, t, 0:UNIT_COLS], in_=w_rows[0][:, t, 0:UNIT_COLS])
         for g in range(1, PASSES):
             load_bytes(0, g, 0, UNIT_COLS)
+        for g in range(PASSES // 2):
+            load_bytes(0, g, UNIT_COLS, LOAD_COLS)
         x_rows = []
         for m in range(BATCH):
             x_tile = const.tile([P, K], BF16, name="x_rows%d" % m, tag="x_rows%d" % m)
             nc.sync.dma_start(out=x_tile[:], in_=x[m])
             x_rows.append(x_tile)
-        for g in range(PASSES):
+        for g in range(PASSES // 2, PASSES):
             load_bytes(0, g, UNIT_COLS, LOAD_COLS)
         for g in range(PASSES):
             new_byte_tile(1, g)
@@ -286,50 +290,43 @@ def tile_improvedattention_pa_kernel(tc, x, W_bytes, W_scale, b, out_0, out_1, o
             for unit, plane in scalar_group(number):
                 widen(unit, plane, False)
 
-        table_s = const.tile([P, 3, D], F32, name="table_s", tag="table_s")
-        table_d = const.tile([P, 3, D], F32, name="table_d", tag="table_d")
-        cross_s = const.tile([P, 2, HALF_D], F32, name="cross_s", tag="cross_s")
-        cross_d = const.tile([P, 2, HALF_D], F32, name="cross_d", tag="cross_d")
-        tables = ((table_s, cross_s, float(D)), (table_d, cross_d, 1.0))
-        for table, cross, step in tables:
-            nc.vector.memset(table[:, :, 0:1], 0.0)
-        for table, cross, step in tables:
-            nc.vector.memset(table[:, 1, 0:1], 1.0)
-        for level in range(7):
+        tables = const.tile([P, 2, TABLE_ROWS + DOUBLINGS, D], F32, name="tables", tag="tables")
+        cross = const.tile([P, 2, TABLE_ROWS + DOUBLINGS - 1, HALF_D], F32, name="cross", tag="cross")
+        table_s, table_d = tables[:, 0], tables[:, 1]
+        steps = (float(D), 1.0)
+        nc.vector.memset(tables[:, :, :, 0:1], 0.0)
+        nc.vector.memset(tables[:, :, 1:TABLE_ROWS + DOUBLINGS:4, 0:1], 1.0)
+        nc.vector.memset(tables[:, :, 3:TABLE_ROWS + DOUBLINGS:4, 0:1], -1.0)
+        for level in range(DOUBLINGS):
             w = 1 << level
-            for table, cross, step in tables:
+            rows = TABLE_ROWS + DOUBLINGS - 1 - level
+            for j in range(2):
                 nc.vector.tensor_scalar(
-                    out=cross[:, :, 0:w], in0=table[:, 1:3, 0:w],
-                    scalar1=math.sin(step * w), scalar2=None, op0=ALU.mult,
+                    out=cross[:, j, 0:rows, 0:w], in0=tables[:, j, 1:rows + 1, 0:w],
+                    scalar1=math.sin(steps[j] * w), scalar2=None, op0=ALU.mult,
                 )
-            for table, cross, step in tables:
+            for j in range(2):
                 nc.vector.scalar_tensor_tensor(
-                    out=table[:, 0:2, w:2 * w], in0=table[:, 0:2, 0:w], scalar=math.cos(step * w),
-                    in1=cross[:, :, 0:w], op0=ALU.mult, op1=ALU.add,
-                )
-            for table, cross, step in tables:
-                nc.vector.tensor_scalar(
-                    out=table[:, 2, w:2 * w], in0=table[:, 0, w:2 * w],
-                    scalar1=-1.0, scalar2=None, op0=ALU.mult,
+                    out=tables[:, j, 0:rows, w:2 * w], in0=tables[:, j, 0:rows, 0:w], scalar=math.cos(steps[j] * w),
+                    in1=cross[:, j, 0:rows, 0:w], op0=ALU.mult, op1=ALU.add,
                 )
 
-        sin_d, cos_d, neg_sin_d = table_d[:, 0, :], table_d[:, 1, :], table_d[:, 2, :]
-        lo, hi = slice(0, HALF_D), slice(HALF_D, D)
-        off_1 = const.tile([P, D], F32, name="off_1", tag="off_1")
-        off_2 = const.tile([P, D], F32, name="off_2", tag="off_2")
-        nc.vector.tensor_tensor(out=r1_r2[:, 0:D], in0=ident[:], in1=cos_d, op=ALU.mult)
-        nc.vector.tensor_tensor(out=off_1[:, lo], in0=ident[:, hi], in1=neg_sin_d[:, lo], op=ALU.mult)
-        nc.vector.tensor_tensor(out=off_1[:, hi], in0=ident[:, lo], in1=sin_d[:, hi], op=ALU.mult)
-        nc.vector.tensor_tensor(out=r1_r2[:, D:2 * D], in0=ident[:], in1=neg_sin_d, op=ALU.mult)
-        nc.vector.tensor_tensor(out=off_2[:, lo], in0=ident[:, hi], in1=cos_d[:, lo], op=ALU.mult)
-        nc.vector.tensor_tensor(out=off_2[:, hi], in0=ident[:, lo], in1=cos_d[:, hi], op=ALU.mult)
-        nc.vector.tensor_tensor(out=r1_r2[:, 0:D], in0=r1_r2[:, 0:D], in1=off_1[:], op=ALU.add)
-        nc.vector.tensor_tensor(
-            out=r1_r2[:, D:D + HALF_D], in0=r1_r2[:, D:D + HALF_D], in1=off_2[:, lo], op=ALU.subtract,
-        )
-        nc.vector.tensor_tensor(
-            out=r1_r2[:, D + HALF_D:2 * D], in0=r1_r2[:, D + HALF_D:2 * D], in1=off_2[:, hi], op=ALU.add,
-        )
+        def build_r1_r2():
+            lo, hi = slice(0, HALF_D), slice(HALF_D, D)
+            both = r1_r2[:].rearrange("p (z d) -> p z d", z=2)
+            off = const.tile([P, 2, D], F32, name="off", tag="off")
+            nc.vector.tensor_tensor(
+                out=both, in0=ident[:].unsqueeze(1).to_broadcast([P, 2, D]), in1=table_d[:, 1:3, :], op=ALU.mult,
+            )
+            nc.vector.tensor_tensor(
+                out=off[:, :, lo], in0=ident[:, hi].unsqueeze(1).to_broadcast([P, 2, HALF_D]),
+                in1=table_d[:, 2:4, lo], op=ALU.mult,
+            )
+            nc.vector.tensor_tensor(
+                out=off[:, :, hi], in0=ident[:, lo].unsqueeze(1).to_broadcast([P, 2, HALF_D]),
+                in1=table_d[:, 0:2, hi], op=ALU.mult,
+            )
+            nc.vector.tensor_tensor(out=both, in0=both, in1=off[:], op=ALU.add)
 
         b_turned = psum.tile([P, 2 * 2 * STRIP_COLS], BF16, name="mx", tag="mx")
         nc.tensor.transpose(b_turned[:, 0:P], b_rows[:], ident_b[:])
@@ -347,8 +344,6 @@ def tile_improvedattention_pa_kernel(tc, x, W_bytes, W_scale, b, out_0, out_1, o
                     nc.tensor.transpose(bank[:, i * P:(i + 1) * P], words[:, 256 * g + u:256 * (g + 1):2], ident[:])
                 x_banks.append(bank)
 
-        nc.vector.tensor_copy(out=bias_col[:], in_=b_turned[:, 0:ROPE_HEADS])
-        nc.vector.tensor_copy(out=sin_cos_s[:], in_=s_turned[:, 0:2 * P:P])
         for plane in vector_planes(0):
             widen(0, plane, True)
 
@@ -380,7 +375,10 @@ def tile_improvedattention_pa_kernel(tc, x, W_bytes, W_scale, b, out_0, out_1, o
 
             if k < N_STRIPS:
                 interleave(k, "vector")
-            if k == 0:
+            if k == 1:
+                build_r1_r2()
+                nc.vector.tensor_copy(out=bias_col[:], in_=b_turned[:, 0:ROPE_HEADS])
+                nc.vector.tensor_copy(out=sin_cos_s[:], in_=s_turned[:, 0:2 * P:P])
                 quantize_x()
             if 0 <= scaled < ROPE_STRIPS:
                 scale_p(scaled)
@@ -403,5 +401,7 @@ def tile_improvedattention_pa_kernel(tc, x, W_bytes, W_scale, b, out_0, out_1, o
 
             if 0 <= biased < ROPE_STRIPS:
                 rotate_by_d(biased)
-            if k < N_STRIPS:
+            if k == 1:
+                mx_matmuls(0)
+            if 1 <= k < N_STRIPS:
                 mx_matmuls(k)

@@ -49,7 +49,7 @@ def vector_planes(unit):
 
 def gpsimd_columns(strip):
     if 4 <= strip <= 19:
-        return 64
+        return 80
     return 0
 
 
@@ -344,18 +344,21 @@ def tile_improvedattention_pa_kernel(tc, x, W_bytes, W_scale, b, out_0, out_1, o
                     nc.tensor.transpose(bank[:, i * P:(i + 1) * P], words[:, 256 * g + u:256 * (g + 1):2], ident[:])
                 x_banks.append(bank)
 
+        build_r1_r2()
         for plane in vector_planes(0):
             widen(0, plane, True)
 
-        def quantize_x():
-            x_grouped = const.tile([P, PACK * PASSES * TOKENS], BF16, name="x_grouped", tag="x_grouped", align_bytes=64)
+        x_grouped = const.tile([P, PACK * PASSES * TOKENS], BF16, name="x_grouped", tag="x_grouped", align_bytes=64)
+
+        def copy_x(m, copy):
             as_words = x_grouped[:].bitcast(F32).rearrange("p (g m r u) -> p g m r u", g=PASSES, m=BATCH, u=2)
-            for m in range(BATCH):
-                for pair in range(PASSES // 2):
-                    nc.vector.tensor_copy(
-                        out=as_words[:, 2 * pair:2 * pair + 2, m, :, :],
-                        in_=x_banks[m * 2 + pair][:].rearrange("p (g u r) -> p g r u", g=2, u=2),
-                    )
+            for pair in range(PASSES // 2):
+                copy(
+                    out=as_words[:, 2 * pair:2 * pair + 2, m, :, :],
+                    in_=x_banks[m * 2 + pair][:].rearrange("p (g u r) -> p g r u", g=2, u=2),
+                )
+
+        def quantize_x():
             x_mx["codes"] = const.tile([P, PASSES * TOKENS], U32, name="x_codes", tag="x_codes", align_bytes=64)
             x_mx["scales"] = const.tile([P, PASSES * TOKENS], U8, name="x_scales", tag="x_scales", align_bytes=64)
             nc.vector.quantize_mx(out=x_mx["codes"][:].bitcast(FP8X4), scales=x_mx["scales"][:], in_=x_grouped[:])
@@ -367,6 +370,8 @@ def tile_improvedattention_pa_kernel(tc, x, W_bytes, W_scale, b, out_0, out_1, o
 
             if k < N_STRIPS:
                 interleave(k, "scalar")
+            if k == 0:
+                copy_x(1, nc.scalar.copy)
             for unit, plane in scalar_group(k + LEAD):
                 widen(unit, plane, False)
 
@@ -376,9 +381,9 @@ def tile_improvedattention_pa_kernel(tc, x, W_bytes, W_scale, b, out_0, out_1, o
             if k < N_STRIPS:
                 interleave(k, "vector")
             if k == 1:
-                build_r1_r2()
                 nc.vector.tensor_copy(out=bias_col[:], in_=b_turned[:, 0:ROPE_HEADS])
                 nc.vector.tensor_copy(out=sin_cos_s[:], in_=s_turned[:, 0:2 * P:P])
+                copy_x(0, nc.vector.tensor_copy)
                 quantize_x()
             if 0 <= scaled < ROPE_STRIPS:
                 scale_p(scaled)

@@ -36,6 +36,7 @@ BYTE_TILES = 3 * PASSES
 GROUP = PLANES // 2
 DOUBLINGS = 7
 TABLE_ROWS = 4
+PLANE_PITCH = UNIT_COLS + 8
 LEAD = 3
 
 FLOPS = 2 * TOKENS * K * N_ALL
@@ -140,9 +141,9 @@ def tile_improvedattention_pa_kernel(tc, x, W_bytes, W_scale, b, out_0, out_1, o
             load, half = divmod(unit, LOAD_COLS // UNIT_COLS)
             g, t = divmod(plane, PACK)
             if unit not in planes_of:
-                planes_of[unit] = stage.tile([P, PLANES, UNIT_COLS], BF16, name="planes", tag="planes")
+                planes_of[unit] = stage.tile([P, PLANES, PLANE_PITCH], BF16, name="planes", tag="planes")
             src = w_bytes_of[(load, g)][:, t, half * UNIT_COLS:(half + 1) * UNIT_COLS].bitcast(FP8)
-            dst = planes_of[unit][:, plane, :]
+            dst = planes_of[unit][:, plane, 0:UNIT_COLS]
             if on_vector:
                 nc.vector.tensor_scalar(
                     out=dst, in0=src, scalar1=w_scale[:, plane:plane + 1], scalar2=None, op0=ALU.mult,

@@ -36,7 +36,7 @@ BYTE_TILES = 3 * PASSES
 GROUP = PLANES // 2
 DOUBLINGS = 7
 TABLE_ROWS = 4
-PLANE_PITCH = UNIT_COLS + 8
+PLANE_PITCH = UNIT_COLS + 40
 LEAD = 3
 
 FLOPS = 2 * TOKENS * K * N_ALL

@@ -50,7 +50,9 @@ def vector_planes(unit):
 
 def gpsimd_columns(strip):
     if 4 <= strip <= 19:
-        return 80
+        return 76
+    if strip > 19:
+        return 16
     return 0
 
 
@@ -175,13 +177,15 @@ def tile_improvedattention_pa_kernel(tc, x, W_bytes, W_scale, b, out_0, out_1, o
                 )
             elif engine == "scalar":
                 if scalar_columns(strip):
+                    first = STRIP_COLS - scalar_columns(strip)
                     nc.scalar.copy(
-                        out=dst[:, :, split:STRIP_COLS, :].rearrange("p g (c i) t -> p g c t i", i=4),
-                        in_=src[:, :, split:STRIP_COLS, :].rearrange("p g (c i) t -> p g c t i", i=4),
+                        out=dst[:, :, first:STRIP_COLS, :].rearrange("p g (c i) t -> p g c t i", i=4),
+                        in_=src[:, :, first:STRIP_COLS, :].rearrange("p g (c i) t -> p g c t i", i=4),
                     )
             elif gpsimd_columns(strip):
                 nc.gpsimd.tensor_scalar(
-                    out=dst[:, :, split:STRIP_COLS, :], in0=src[:, :, split:STRIP_COLS, :],
+                    out=dst[:, :, split:split + gpsimd_columns(strip), :],
+                    in0=src[:, :, split:split + gpsimd_columns(strip), :],
                     scalar1=1.0, scalar2=0.0, op0=ALU.mult, op1=ALU.add,
                 )
 
@@ -392,13 +396,15 @@ def tile_improvedattention_pa_kernel(tc, x, W_bytes, W_scale, b, out_0, out_1, o
                 add_bias_transposed(biased)
             if 0 <= scaled < ROPE_STRIPS:
                 add_scaled_q(scaled)
-            if ROPE_STRIPS <= v_done < N_STRIPS:
+            if ROPE_STRIPS <= v_done < N_STRIPS and k != N_STRIPS - 1:
                 add_bias_v(v_done)
             if k % 2 == 0 and k // 2 + 1 < N_UNITS:
                 for plane in vector_planes(k // 2 + 1):
                     widen(k // 2 + 1, plane, True)
             if k < N_STRIPS:
                 quantize(k)
+            if k == N_STRIPS - 1:
+                add_bias_v(v_done)
 
             if k % 4 == 0 and k // 4 + 3 < N_LOADS:
                 for g in range(PASSES):

@@ -83,6 +83,7 @@ def tile_improvedattention_pa_kernel(tc, x, W_bytes, W_scale, b, out_0, out_1, o
         codes_of = {}
         scales_of = {}
         sums_of = {}
+        groups_of = {}
         u_t_of = {}
         pq_of = {}
         p_scaled_of = {}
@@ -198,6 +199,11 @@ def tile_improvedattention_pa_kernel(tc, x, W_bytes, W_scale, b, out_0, out_1, o
 
         def mx_matmuls(strip):
             sums_of[strip] = psum.tile([P, 2 * STRIP_COLS], F32, name="mx", tag="mx")
+            group_out = [sums_of[strip][:, i * STRIP_COLS:(i + 1) * STRIP_COLS] for i in range(2)]
+            if strip == N_STRIPS - 1:
+                last_sums = psum.tile([P, 2 * STRIP_COLS], F32, name="mx", tag="mx")
+                group_out[1] = last_sums[:, 0:STRIP_COLS]
+            groups_of[strip] = group_out
             w_c, w_s = codes_of[strip], scales_of[strip]
             for i in range(2):
                 for g in range(PASSES):
@@ -208,7 +214,7 @@ def tile_improvedattention_pa_kernel(tc, x, W_bytes, W_scale, b, out_0, out_1, o
                         lhs_c, lhs_s, lhs_cols = x_mx["codes"], x_mx["scales"], slice(g * TOKENS + i * P, g * TOKENS + (i + 1) * P)
                         rhs_c, rhs_s, rhs_cols = w_c, w_s, slice(g * STRIP_COLS, (g + 1) * STRIP_COLS)
                     nc.tensor.matmul_mx(
-                        out=sums_of[strip][:, i * STRIP_COLS:(i + 1) * STRIP_COLS],
+                        out=group_out[i],
                         lhsT=lhs_c[:, lhs_cols].bitcast(FP8X4),
                         lhsT_scale=lhs_s[:, lhs_cols],
                         rhs=rhs_c[:, rhs_cols].bitcast(FP8X4),
@@ -233,9 +239,9 @@ def tile_improvedattention_pa_kernel(tc, x, W_bytes, W_scale, b, out_0, out_1, o
         def rotate_by_d(strip):
             pq_of[(strip, 0)] = psum.tile([P, 2 * STRIP_COLS], F32, name="pq", tag="pq")
             pq_of[(strip, 1)] = psum.tile([P, 2 * STRIP_COLS], F32, name="pq", tag="pq")
-            for i in range(2):
-                for m in range(BATCH):
-                    for z in range(2):
+            for z in range(2):
+                for i in range(2):
+                    for m in range(BATCH):
                         nc.tensor.matmul(
                             out=pq_of[(strip, z)][:, m * STRIP_COLS + i * D:m * STRIP_COLS + (i + 1) * D],
                             lhsT=u_t_of[strip][:, i * TOKENS + m * P:i * TOKENS + (m + 1) * P],
@@ -257,10 +263,10 @@ def tile_improvedattention_pa_kernel(tc, x, W_bytes, W_scale, b, out_0, out_1, o
                 out_tile_of[number] = epi.tile([P, BATCH, LOAD_COLS], F32, name="out_tile", tag="out_tile", bufs=3)
             return out_tile_of[number]
 
-        def store(strip, c0, c1):
+        def store(strip, c0, c1, entries=(0, 1)):
             number = strip // STRIPS_PER_STORE
             first_col = (number % 2) * LOAD_COLS
-            for m in range(BATCH):
+            for m in entries:
                 nc.sync.dma_start(
                     out=outs[number // 2][m][:, first_col + c0:first_col + c1], in_=out_tile_of[number][:, m, c0:c1],
                 )
@@ -280,6 +286,14 @@ def tile_improvedattention_pa_kernel(tc, x, W_bytes, W_scale, b, out_0, out_1, o
         def add_bias_v(strip):
             first_col = (strip % STRIPS_PER_STORE) * STRIP_COLS
             v_col = (strip - ROPE_STRIPS) * STRIP_COLS
+            if strip == N_STRIPS - 1:
+                for m in range(BATCH):
+                    nc.vector.tensor_tensor(
+                        out=out_tile(strip)[:, m, first_col:first_col + STRIP_COLS], in0=groups_of[strip][m],
+                        in1=bias_v[:, v_col:v_col + STRIP_COLS], op=ALU.add,
+                    )
+                    store(strip, first_col, first_col + STRIP_COLS, [m])
+                return
             nc.vector.tensor_tensor(
                 out=out_tile(strip)[:, :, first_col:first_col + STRIP_COLS],
                 in0=sums_of[strip][:].rearrange("p (m c) -> p m c", m=BATCH),

@@ -389,9 +389,9 @@ def tile_improvedattention_pa_kernel(tc, x, W_bytes, W_scale, b, out_0, out_1, o
 
             if k < N_STRIPS:
                 interleave(k, "scalar")
-            if k == 0:
-                copy_x(1, nc.scalar.copy)
-            for unit, plane in scalar_group(k + LEAD):
+            for number, (unit, plane) in enumerate(scalar_group(k + LEAD)):
+                if k == 0 and number == GROUP // 2:
+                    copy_x(0, nc.scalar.copy)
                 widen(unit, plane, False)
 
             if k + 1 < N_STRIPS:
@@ -402,7 +402,7 @@ def tile_improvedattention_pa_kernel(tc, x, W_bytes, W_scale, b, out_0, out_1, o
             if k == 1:
                 nc.vector.tensor_copy(out=bias_col[:], in_=b_turned[:, 0:ROPE_HEADS])
                 nc.vector.tensor_copy(out=sin_cos_s[:], in_=s_turned[:, 0:2 * P:P])
-                copy_x(0, nc.vector.tensor_copy)
+                copy_x(1, nc.vector.tensor_copy)
                 quantize_x()
             if 0 <= scaled < ROPE_STRIPS:
                 scale_p(scaled)

@@ -39,12 +39,16 @@ TABLE_ROWS = 4
 PLANE_PITCH = UNIT_COLS + 40
 LEAD = 3
 
+EARLY_COPIES = (1, N_STRIPS - 1)
+
 FLOPS = 2 * TOKENS * K * N_ALL
 
 
 def vector_planes(unit):
     if unit == 0:
         return list(range(PLANES - 10, PLANES))
+    if unit == 2:
+        return [PLANES - 1]
     return []
 
 
@@ -397,26 +401,32 @@ def tile_improvedattention_pa_kernel(tc, x, W_bytes, W_scale, b, out_0, out_1, o
             if k + 1 < N_STRIPS:
                 interleave(k + 1, "gpsimd")
 
-            if k < N_STRIPS:
+            if k < N_STRIPS and k not in EARLY_COPIES:
                 interleave(k, "vector")
             if k == 1:
                 nc.vector.tensor_copy(out=bias_col[:], in_=b_turned[:, 0:ROPE_HEADS])
                 nc.vector.tensor_copy(out=sin_cos_s[:], in_=s_turned[:, 0:2 * P:P])
                 copy_x(1, nc.vector.tensor_copy)
-                quantize_x()
+            v_between = ROPE_STRIPS <= v_done < N_STRIPS and 0 <= scaled < ROPE_STRIPS <= biased
             if 0 <= scaled < ROPE_STRIPS:
                 scale_p(scaled)
             if 0 <= biased < ROPE_STRIPS:
                 add_bias_transposed(biased)
+            if v_between:
+                add_bias_v(v_done)
             if 0 <= scaled < ROPE_STRIPS:
                 add_scaled_q(scaled)
-            if ROPE_STRIPS <= v_done < N_STRIPS and k != N_STRIPS - 1:
+            if ROPE_STRIPS <= v_done < N_STRIPS and k != N_STRIPS - 1 and not v_between:
                 add_bias_v(v_done)
             if k % 2 == 0 and k // 2 + 1 < N_UNITS:
                 for plane in vector_planes(k // 2 + 1):
                     widen(k // 2 + 1, plane, True)
+            if k + 1 in EARLY_COPIES:
+                interleave(k + 1, "vector")
             if k < N_STRIPS:
                 quantize(k)
+            if k == 1:
+                quantize_x()
             if k == N_STRIPS - 1:
                 add_bias_v(v_done)
 

@@ -57,7 +57,15 @@ def gpsimd_columns(strip):
         return 76
     if strip > 19:
         return 16
+    if strip == 2:
+        return 96
     return 0
+
+
+def gpsimd_passes(strip):
+    if strip == 2:
+        return PASSES // 2
+    return PASSES
 
 
 def scalar_columns(strip):
@@ -175,11 +183,18 @@ def tile_improvedattention_pa_kernel(tc, x, W_bytes, W_scale, b, out_0, out_1, o
             split = STRIP_COLS - gpsimd_columns(strip) - scalar_columns(strip)
             dst = grouped_of[strip][:].rearrange("p (g c t) -> p g c t", g=PASSES, t=PACK)
             src = planes_of[unit][:, :, sub * STRIP_COLS:(sub + 1) * STRIP_COLS].rearrange("p (g t) c -> p g c t", t=PACK)
+            shared = gpsimd_passes(strip)
             if engine == "vector":
                 nc.vector.tensor_copy(
-                    out=dst[:, :, 0:split, :].rearrange("p g (c i) t -> p g c t i", i=4),
-                    in_=src[:, :, 0:split, :].rearrange("p g (c i) t -> p g c t i", i=4),
+                    out=dst[:, 0:shared, 0:split, :].rearrange("p g (c i) t -> p g c t i", i=4),
+                    in_=src[:, 0:shared, 0:split, :].rearrange("p g (c i) t -> p g c t i", i=4),
                 )
+                if shared < PASSES:
+                    whole = split + gpsimd_columns(strip)
+                    nc.vector.tensor_copy(
+                        out=dst[:, shared:PASSES, 0:whole, :].rearrange("p g (c i) t -> p g c t i", i=4),
+                        in_=src[:, shared:PASSES, 0:whole, :].rearrange("p g (c i) t -> p g c t i", i=4),
+                    )
             elif engine == "scalar":
                 if scalar_columns(strip):
                     first = STRIP_COLS - scalar_columns(strip)
@@ -189,8 +204,8 @@ def tile_improvedattention_pa_kernel(tc, x, W_bytes, W_scale, b, out_0, out_1, o
                     )
             elif gpsimd_columns(strip):
                 nc.gpsimd.tensor_scalar(
-                    out=dst[:, :, split:split + gpsimd_columns(strip), :],
-                    in0=src[:, :, split:split + gpsimd_columns(strip), :],
+                    out=dst[:, 0:shared, split:split + gpsimd_columns(strip), :],
+                    in0=src[:, 0:shared, split:split + gpsimd_columns(strip), :],
                     scalar1=1.0, scalar2=0.0, op0=ALU.mult, op1=ALU.add,
                 )
 

@@ -41,6 +41,8 @@ LEAD = 3
 
 EARLY_COPIES = (1, N_STRIPS - 1)
 
+IDLE_PASSES = {19: 6, 20: 6, 21: 8}
+
 FLOPS = 2 * TOKENS * K * N_ALL
 
 
@@ -241,6 +243,19 @@ def tile_improvedattention_pa_kernel(tc, x, W_bytes, W_scale, b, out_0, out_1, o
                         start=(g == 0),
                         stop=(g == PASSES - 1),
                     )
+
+        def keep_clock_up(strip, passes):
+            idle_bank = psum.tile([P, 2 * STRIP_COLS], F32, name="pq", tag="pq")
+            for unused in range(passes):
+                nc.tensor.matmul_mx(
+                    out=idle_bank[:],
+                    lhsT=x_mx["codes"][:, 0:P].bitcast(FP8X4),
+                    lhsT_scale=x_mx["scales"][:, 0:P],
+                    rhs=codes_of[strip][:, 0:2 * STRIP_COLS].bitcast(FP8X4),
+                    rhs_scale=scales_of[strip][:, 0:2 * STRIP_COLS],
+                    start=True,
+                    stop=True,
+                )
 
         bias_col = const.tile([P, ROPE_HEADS], F32, name="bias_col", tag="bias_col")
         sin_cos_s = const.tile([P, 2], F32, name="sin_cos_s", tag="sin_cos_s")
@@ -456,3 +471,5 @@ def tile_improvedattention_pa_kernel(tc, x, W_bytes, W_scale, b, out_0, out_1, o
                 mx_matmuls(0)
             if 1 <= k < N_STRIPS:
                 mx_matmuls(k)
+            if k in IDLE_PASSES:
+                keep_clock_up(k, IDLE_PASSES[k])

@@ -434,9 +434,10 @@ def tile_improvedattention_pa_kernel(tc, x, W_bytes, W_scale, b, out_0, out_1, o
             if k < N_STRIPS and k not in EARLY_COPIES:
                 interleave(k, "vector")
             if k == 1:
+                copy_x(1, nc.vector.tensor_copy)
                 nc.vector.tensor_copy(out=bias_col[:], in_=b_turned[:, 0:ROPE_HEADS])
                 nc.vector.tensor_copy(out=sin_cos_s[:], in_=s_turned[:, 0:2 * P:P])
-                copy_x(1, nc.vector.tensor_copy)
+                quantize_x()
             v_between = ROPE_STRIPS <= v_done < N_STRIPS and 0 <= scaled < ROPE_STRIPS <= biased
             if 0 <= scaled < ROPE_STRIPS:
                 scale_p(scaled)
@@ -455,8 +456,6 @@ def tile_improvedattention_pa_kernel(tc, x, W_bytes, W_scale, b, out_0, out_1, o
                 interleave(k + 1, "vector")
             if k < N_STRIPS:
                 quantize(k)
-            if k == 1:
-                quantize_x()
             if k == N_STRIPS - 1:
                 add_bias_v(v_done)
 

@@ -50,7 +50,7 @@ def vector_planes(unit):
     if unit == 0:
         return list(range(PLANES - 10, PLANES))
     if unit == 2:
-        return [PLANES - 1]
+        return [PLANES - 2, PLANES - 1]
     return []
 
 

import math
from contextlib import ExitStack

import concourse.mybir as mybir
from concourse.masks import make_identity

F32 = mybir.dt.float32
BF16 = mybir.dt.bfloat16
U32 = mybir.dt.uint32
U8 = mybir.dt.uint8
FP8 = mybir.dt.float8_e4m3fn
FP8X4 = mybir.dt.float8_e4m3fn_x4
ALU = mybir.AluOpType
ACT = mybir.ActivationFunctionType

P = 128
PACK = 4
K = 2048
PASSES = K // (P * PACK)
PLANES = PASSES * PACK
N_ALL = 6144
BATCH = 2
TOKENS = BATCH * P
D = 128
HALF_D = D // 2
LOAD_COLS = 1024
UNIT_COLS = 512
STRIP_COLS = 256
N_LOADS = N_ALL // LOAD_COLS
N_UNITS = N_ALL // UNIT_COLS
N_STRIPS = N_ALL // STRIP_COLS
ROPE_STRIPS = 2 * K // STRIP_COLS
ROPE_HEADS = 2 * ROPE_STRIPS
STRIPS_PER_STORE = LOAD_COLS // STRIP_COLS
BYTE_TILES = 3 * PASSES
GROUP = PLANES // 2
DOUBLINGS = 7
TABLE_ROWS = 4
PLANE_PITCH = UNIT_COLS + 40
LEAD = 3

EARLY_COPIES = (1, N_STRIPS - 1)

IDLE_PASSES = {19: 6, 20: 6, 21: 8}

FLOPS = 2 * TOKENS * K * N_ALL


def vector_planes(unit):
    if unit == 0:
        return list(range(PLANES - 10, PLANES))
    if unit == 2:
        return [PLANES - 2, PLANES - 1]
    return []


def gpsimd_columns(strip):
    if 4 <= strip <= 19:
        return 76
    if strip > 19:
        return 16
    if strip == 2:
        return 96
    return 0


def gpsimd_passes(strip):
    if strip == 2:
        return PASSES // 2
    return PASSES


def scalar_columns(strip):
    if strip >= N_STRIPS - 2:
        return 128
    if strip > 19:
        return 64
    return 0


def tile_improvedattention_pa_kernel(tc, x, W_bytes, W_scale, b, out_0, out_1, out_2):
    nc = tc.nc
    outs = [o.rearrange("b s h d -> b s (h d)") for o in (out_0, out_1, out_2)]
    w_rows = W_bytes.rearrange("(g p t) n -> g p t n", p=P, t=PACK)

    with ExitStack() as ctx:
        const = ctx.enter_context(tc.tile_pool(name="const", bufs=1))
        byte_pool = ctx.enter_context(tc.tile_pool(name="byte_pool", bufs=BYTE_TILES))
        stage = ctx.enter_context(tc.tile_pool(name="stage", bufs=3))
        epi = ctx.enter_context(tc.tile_pool(name="epi", bufs=4))
        psum = ctx.enter_context(tc.psum_pool(name="psum", bufs=4))
        ctx.enter_context(tc.manual_schedule())

        w_bytes_of = {}
        planes_of = {}
        grouped_of = {}
        codes_of = {}
        scales_of = {}
        sums_of = {}
        groups_of = {}
        u_t_of = {}
        pq_of = {}
        p_scaled_of = {}
        out_tile_of = {}
        x_mx = {}

        w_scale = const.tile([P, PLANES], F32, name="w_scale", tag="w_scale")
        nc.scalar.dma_start(
            out=w_scale[:].rearrange("p (g t) -> p g t", t=PACK),
            in_=W_scale.rearrange("(g p t) o -> p g (t o)", p=P, t=PACK),
        )
        warm_in = const.tile([P, 1], F32, name="warm_in", tag="warm_in")
        warm_out = const.tile([P, 1], F32, name="warm_out", tag="warm_out")
        nc.gpsimd.memset(warm_in[:], 0.0)
        b_rows = const.tile([P, D], BF16, name="b_rows", tag="b_rows")
        nc.gpsimd.memset(b_rows[:], 0.0)
        nc.scalar.dma_start(out=b_rows[0:ROPE_HEADS, :], in_=b[0:ROPE_HEADS * D].rearrange("(h d) -> h d", d=D))
        nc.scalar.activation(out=warm_out[:], in_=warm_in[:], func=ACT.Copy)
        ident_b = const.tile([P, P], BF16, name="ident_b", tag="ident_b")
        make_identity(nc, ident_b[:])
        ident = const.tile([P, P], F32, name="ident", tag="ident")
        make_identity(nc, ident[:])

        def new_byte_tile(load, g):
            w_bytes_of[(load, g)] = byte_pool.tile([P, PACK, LOAD_COLS], U8, name="w_bytes", tag="w_bytes")

        def load_bytes(load, g, c0, c1):
            nc.sync.dma_start(
                out=w_bytes_of[(load, g)][:, :, c0:c1],
                in_=w_rows[g][:, :, load * LOAD_COLS + c0:load * LOAD_COLS + c1],
            )

        for g in range(PASSES):
            new_byte_tile(0, g)
        for t in range(PACK):
            nc.sync.dma_start(out=w_bytes_of[(0, 0)][:, t, 0:UNIT_COLS], in_=w_rows[0][:, t, 0:UNIT_COLS])
        for g in range(1, PASSES):
            load_bytes(0, g, 0, UNIT_COLS)
        for g in range(PASSES // 2):
            load_bytes(0, g, UNIT_COLS, LOAD_COLS)
        x_rows = []
        for m in range(BATCH):
            x_tile = const.tile([P, K], BF16, name="x_rows%d" % m, tag="x_rows%d" % m)
            nc.sync.dma_start(out=x_tile[:], in_=x[m])
            x_rows.append(x_tile)
        for g in range(PASSES // 2, PASSES):
            load_bytes(0, g, UNIT_COLS, LOAD_COLS)
        for g in range(PASSES):
            new_byte_tile(1, g)
            load_bytes(1, g, 0, LOAD_COLS)
        bias_v = const.tile([P, K], BF16, name="bias_v", tag="bias_v")
        nc.sync.dma_start(out=bias_v[:], in_=b[2 * K:3 * K].partition_broadcast(P))
        for g in range(PASSES):
            new_byte_tile(2, g)
            load_bytes(2, g, 0, LOAD_COLS)

        def widen(unit, plane, on_vector):
            load, half = divmod(unit, LOAD_COLS // UNIT_COLS)
            g, t = divmod(plane, PACK)
            if unit not in planes_of:
                planes_of[unit] = stage.tile([P, PLANES, PLANE_PITCH], BF16, name="planes", tag="planes")
            src = w_bytes_of[(load, g)][:, t, half * UNIT_COLS:(half + 1) * UNIT_COLS].bitcast(FP8)
            dst = planes_of[unit][:, plane, 0:UNIT_COLS]
            if on_vector:
                nc.vector.tensor_scalar(
                    out=dst, in0=src, scalar1=w_scale[:, plane:plane + 1], scalar2=None, op0=ALU.mult,
                )
            else:
                nc.scalar.activation(out=dst, in_=src, func=ACT.Copy, scale=w_scale[:, plane:plane + 1])

        def scalar_group(number):
            unit, part = divmod(number, 2)
            if unit >= N_UNITS:
                return []
            return [
                (unit, plane) for plane in range(part * GROUP, (part + 1) * GROUP) if plane not in vector_planes(unit)
            ]

        def interleave(strip, engine):
            unit, sub = divmod(strip, UNIT_COLS // STRIP_COLS)
            if strip not in grouped_of:
                grouped_of[strip] = stage.tile(
                    [P, PACK * PASSES * STRIP_COLS], BF16, name="grouped", tag="grouped", align_bytes=64, bufs=2,
                )
            split = STRIP_COLS - gpsimd_columns(strip) - scalar_columns(strip)
            dst = grouped_of[strip][:].rearrange("p (g c t) -> p g c t", g=PASSES, t=PACK)
            src = planes_of[unit][:, :, sub * STRIP_COLS:(sub + 1) * STRIP_COLS].rearrange("p (g t) c -> p g c t", t=PACK)
            shared = gpsimd_passes(strip)
            if engine == "vector":
                nc.vector.tensor_copy(
                    out=dst[:, 0:shared, 0:split, :].rearrange("p g (c i) t -> p g c t i", i=4),
                    in_=src[:, 0:shared, 0:split, :].rearrange("p g (c i) t -> p g c t i", i=4),
                )
                if shared < PASSES:
                    whole = split + gpsimd_columns(strip)
                    nc.vector.tensor_copy(
                        out=dst[:, shared:PASSES, 0:whole, :].rearrange("p g (c i) t -> p g c t i", i=4),
                        in_=src[:, shared:PASSES, 0:whole, :].rearrange("p g (c i) t -> p g c t i", i=4),
                    )
            elif engine == "scalar":
                if scalar_columns(strip):
                    first = STRIP_COLS - scalar_columns(strip)
                    nc.scalar.copy(
                        out=dst[:, :, first:STRIP_COLS, :].rearrange("p g (c i) t -> p g c t i", i=4),
                        in_=src[:, :, first:STRIP_COLS, :].rearrange("p g (c i) t -> p g c t i", i=4),
                    )
            elif gpsimd_columns(strip):
                nc.gpsimd.tensor_scalar(
                    out=dst[:, 0:shared, split:split + gpsimd_columns(strip), :],
                    in0=src[:, 0:shared, split:split + gpsimd_columns(strip), :],
                    scalar1=1.0, scalar2=0.0, op0=ALU.mult, op1=ALU.add,
                )

        def quantize(strip):
            codes_of[strip] = stage.tile([P, PASSES * STRIP_COLS], U32, name="codes", tag="codes", align_bytes=64)
            scales_of[strip] = stage.tile([P, PASSES * STRIP_COLS], U8, name="scales", tag="scales", align_bytes=64)
            nc.vector.quantize_mx(
                out=codes_of[strip][:].bitcast(FP8X4), scales=scales_of[strip][:], in_=grouped_of[strip][:],
            )

        def mx_matmuls(strip):
            sums_of[strip] = psum.tile([P, 2 * STRIP_COLS], F32, name="mx", tag="mx")
            group_out = [sums_of[strip][:, i * STRIP_COLS:(i + 1) * STRIP_COLS] for i in range(2)]
            if strip == N_STRIPS - 1:
                last_sums = psum.tile([P, 2 * STRIP_COLS], F32, name="mx", tag="mx")
                group_out[1] = last_sums[:, 0:STRIP_COLS]
            groups_of[strip] = group_out
            w_c, w_s = codes_of[strip], scales_of[strip]
            for i in range(2):
                for g in range(PASSES):
                    if strip < ROPE_STRIPS:
                        lhs_c, lhs_s, lhs_cols = w_c, w_s, slice(g * STRIP_COLS + i * D, g * STRIP_COLS + (i + 1) * D)
                        rhs_c, rhs_s, rhs_cols = x_mx["codes"], x_mx["scales"], slice(g * TOKENS, (g + 1) * TOKENS)
                    else:
                        lhs_c, lhs_s, lhs_cols = x_mx["codes"], x_mx["scales"], slice(g * TOKENS + i * P, g * TOKENS + (i + 1) * P)
                        rhs_c, rhs_s, rhs_cols = w_c, w_s, slice(g * STRIP_COLS, (g + 1) * STRIP_COLS)
                    nc.tensor.matmul_mx(
                        out=group_out[i],
                        lhsT=lhs_c[:, lhs_cols].bitcast(FP8X4),
                        lhsT_scale=lhs_s[:, lhs_cols],
                        rhs=rhs_c[:, rhs_cols].bitcast(FP8X4),
                        rhs_scale=rhs_s[:, rhs_cols],
                        start=(g == 0),
                        stop=(g == PASSES - 1),
                    )

        def keep_clock_up(strip, passes):
            idle_bank = psum.tile([P, 2 * STRIP_COLS], F32, name="pq", tag="pq")
            for unused in range(passes):
                nc.tensor.matmul_mx(
                    out=idle_bank[:],
                    lhsT=x_mx["codes"][:, 0:P].bitcast(FP8X4),
                    lhsT_scale=x_mx["scales"][:, 0:P],
                    rhs=codes_of[strip][:, 0:2 * STRIP_COLS].bitcast(FP8X4),
                    rhs_scale=scales_of[strip][:, 0:2 * STRIP_COLS],
                    start=True,
                    stop=True,
                )

        bias_col = const.tile([P, ROPE_HEADS], F32, name="bias_col", tag="bias_col")
        sin_cos_s = const.tile([P, 2], F32, name="sin_cos_s", tag="sin_cos_s")
        r1_r2 = const.tile([P, 2 * D], F32, name="r1_r2", tag="r1_r2")

        def add_bias_transposed(strip):
            u_t_of[strip] = epi.tile([P, 2 * TOKENS], F32, name="u_t", tag="u_t")
            nc.vector.tensor_tensor(
                out=u_t_of[strip][:].rearrange("p (i n) -> p i n", i=2),
                in0=sums_of[strip][:].rearrange("p (i n) -> p i n", i=2),
                in1=bias_col[:, 2 * strip:2 * strip + 2].unsqueeze(2).to_broadcast([P, 2, TOKENS]),
                op=ALU.add,
            )

        def rotate_by_d(strip):
            pq_of[(strip, 0)] = psum.tile([P, 2 * STRIP_COLS], F32, name="pq", tag="pq")
            pq_of[(strip, 1)] = psum.tile([P, 2 * STRIP_COLS], F32, name="pq", tag="pq")
            for z in range(2):
                for i in range(2):
                    for m in range(BATCH):
                        nc.tensor.matmul(
                            out=pq_of[(strip, z)][:, m * STRIP_COLS + i * D:m * STRIP_COLS + (i + 1) * D],
                            lhsT=u_t_of[strip][:, i * TOKENS + m * P:i * TOKENS + (m + 1) * P],
                            rhs=r1_r2[:, z * D:(z + 1) * D],
                            start=True,
                            stop=True,
                        )

        def scale_p(strip):
            p_scaled_of[strip] = epi.tile([P, 2 * STRIP_COLS], F32, name="p_scaled", tag="p_scaled")
            nc.vector.tensor_scalar(
                out=p_scaled_of[strip][:], in0=pq_of[(strip, 0)][:],
                scalar1=sin_cos_s[:, 1:2], scalar2=None, op0=ALU.mult,
            )

        def out_tile(strip):
            number = strip // STRIPS_PER_STORE
            if number not in out_tile_of:
                out_tile_of[number] = epi.tile([P, BATCH, LOAD_COLS], F32, name="out_tile", tag="out_tile", bufs=3)
            return out_tile_of[number]

        def store(strip, c0, c1, entries=(0, 1)):
            number = strip // STRIPS_PER_STORE
            first_col = (number % 2) * LOAD_COLS
            for m in entries:
                nc.sync.dma_start(
                    out=outs[number // 2][m][:, first_col + c0:first_col + c1], in_=out_tile_of[number][:, m, c0:c1],
                )

        def add_scaled_q(strip):
            first_col = (strip % STRIPS_PER_STORE) * STRIP_COLS
            nc.vector.scalar_tensor_tensor(
                out=out_tile(strip)[:, :, first_col:first_col + STRIP_COLS],
                in0=pq_of[(strip, 1)][:].rearrange("p (m z) -> p m z", m=BATCH),
                scalar=sin_cos_s[:, 0:1],
                in1=p_scaled_of[strip][:].rearrange("p (m z) -> p m z", m=BATCH),
                op0=ALU.mult, op1=ALU.add,
            )
            if strip % STRIPS_PER_STORE == STRIPS_PER_STORE - 1:
                store(strip, 0, LOAD_COLS)

        def add_bias_v(strip):
            first_col = (strip % STRIPS_PER_STORE) * STRIP_COLS
            v_col = (strip - ROPE_STRIPS) * STRIP_COLS
            if strip == N_STRIPS - 1:
                for m in range(BATCH):
                    nc.vector.tensor_tensor(
                        out=out_tile(strip)[:, m, first_col:first_col + STRIP_COLS], in0=groups_of[strip][m],
                        in1=bias_v[:, v_col:v_col + STRIP_COLS], op=ALU.add,
                    )
                    store(strip, first_col, first_col + STRIP_COLS, [m])
                return
            nc.vector.tensor_tensor(
                out=out_tile(strip)[:, :, first_col:first_col + STRIP_COLS],
                in0=sums_of[strip][:].rearrange("p (m c) -> p m c", m=BATCH),
                in1=bias_v[:, v_col:v_col + STRIP_COLS].unsqueeze(1).to_broadcast([P, BATCH, STRIP_COLS]),
                op=ALU.add,
            )
            if strip >= N_STRIPS - STRIPS_PER_STORE:
                store(strip, first_col, first_col + STRIP_COLS)
            elif strip % STRIPS_PER_STORE == STRIPS_PER_STORE - 1:
                store(strip, 0, LOAD_COLS)

        for number in range(LEAD):
            for unit, plane in scalar_group(number):
                widen(unit, plane, False)

        tables = const.tile([P, 2, TABLE_ROWS + DOUBLINGS, D], F32, name="tables", tag="tables")
        cross = const.tile([P, 2, TABLE_ROWS + DOUBLINGS - 1, HALF_D], F32, name="cross", tag="cross")
        table_s, table_d = tables[:, 0], tables[:, 1]
        steps = (float(D), 1.0)
        nc.vector.memset(tables[:, :, :, 0:1], 0.0)
        nc.vector.memset(tables[:, :, 1:TABLE_ROWS + DOUBLINGS:4, 0:1], 1.0)
        nc.vector.memset(tables[:, :, 3:TABLE_ROWS + DOUBLINGS:4, 0:1], -1.0)
        for level in range(DOUBLINGS):
            w = 1 << level
            rows = TABLE_ROWS + DOUBLINGS - 1 - level
            for j in range(2):
                nc.vector.tensor_scalar(
                    out=cross[:, j, 0:rows, 0:w], in0=tables[:, j, 1:rows + 1, 0:w],
                    scalar1=math.sin(steps[j] * w), scalar2=None, op0=ALU.mult,
                )
            for j in range(2):
                nc.vector.scalar_tensor_tensor(
                    out=tables[:, j, 0:rows, w:2 * w], in0=tables[:, j, 0:rows, 0:w], scalar=math.cos(steps[j] * w),
                    in1=cross[:, j, 0:rows, 0:w], op0=ALU.mult, op1=ALU.add,
                )

        def build_r1_r2():
            lo, hi = slice(0, HALF_D), slice(HALF_D, D)
            both = r1_r2[:].rearrange("p (z d) -> p z d", z=2)
            off = const.tile([P, 2, D], F32, name="off", tag="off")
            nc.vector.tensor_tensor(
                out=both, in0=ident[:].unsqueeze(1).to_broadcast([P, 2, D]), in1=table_d[:, 1:3, :], op=ALU.mult,
            )
            nc.vector.tensor_tensor(
                out=off[:, :, lo], in0=ident[:, hi].unsqueeze(1).to_broadcast([P, 2, HALF_D]),
                in1=table_d[:, 2:4, lo], op=ALU.mult,
            )
            nc.vector.tensor_tensor(
                out=off[:, :, hi], in0=ident[:, lo].unsqueeze(1).to_broadcast([P, 2, HALF_D]),
                in1=table_d[:, 0:2, hi], op=ALU.mult,
            )
            nc.vector.tensor_tensor(out=both, in0=both, in1=off[:], op=ALU.add)

        b_turned = psum.tile([P, 2 * 2 * STRIP_COLS], BF16, name="mx", tag="mx")
        nc.tensor.transpose(b_turned[:, 0:P], b_rows[:], ident_b[:])
        s_turned = psum.tile([P, 2 * STRIP_COLS], F32, name="mx", tag="mx")
        nc.tensor.transpose(s_turned[:, 0:P], table_s[:, 0, :], ident[:])
        nc.tensor.transpose(s_turned[:, P:2 * P], table_s[:, 1, :], ident[:])
        x_banks = []
        for m in range(BATCH):
            words = x_rows[m][:].bitcast(F32)
            for pair in range(PASSES // 2):
                bank = psum.tile([P, 2 * STRIP_COLS], F32, name="pq", tag="pq")
                for i in range(4):
                    g = 2 * pair + i // 2
                    u = i % 2
                    nc.tensor.transpose(bank[:, i * P:(i + 1) * P], words[:, 256 * g + u:256 * (g + 1):2], ident[:])
                x_banks.append(bank)

        build_r1_r2()
        for plane in vector_planes(0):
            widen(0, plane, True)

        x_grouped = const.tile([P, PACK * PASSES * TOKENS], BF16, name="x_grouped", tag="x_grouped", align_bytes=64)

        def copy_x(m, copy):
            as_words = x_grouped[:].bitcast(F32).rearrange("p (g m r u) -> p g m r u", g=PASSES, m=BATCH, u=2)
            for pair in range(PASSES // 2):
                copy(
                    out=as_words[:, 2 * pair:2 * pair + 2, m, :, :],
                    in_=x_banks[m * 2 + pair][:].rearrange("p (g u r) -> p g r u", g=2, u=2),
                )

        def quantize_x():
            x_mx["codes"] = const.tile([P, PASSES * TOKENS], U32, name="x_codes", tag="x_codes", align_bytes=64)
            x_mx["scales"] = const.tile([P, PASSES * TOKENS], U8, name="x_scales", tag="x_scales", align_bytes=64)
            nc.vector.quantize_mx(out=x_mx["codes"][:].bitcast(FP8X4), scales=x_mx["scales"][:], in_=x_grouped[:])

        for k in range(N_STRIPS + 2):
            biased = k - 2
            scaled = k - 3
            v_done = k - 2

            if k < N_STRIPS:
                interleave(k, "scalar")
            for number, (unit, plane) in enumerate(scalar_group(k + LEAD)):
                if k == 0 and number == GROUP // 2:
                    copy_x(0, nc.scalar.copy)
                widen(unit, plane, False)

            if k + 1 < N_STRIPS:
                interleave(k + 1, "gpsimd")

            if k < N_STRIPS and k not in EARLY_COPIES:
                interleave(k, "vector")
            if k == 1:
                copy_x(1, nc.vector.tensor_copy)
                nc.vector.tensor_copy(out=bias_col[:], in_=b_turned[:, 0:ROPE_HEADS])
                nc.vector.tensor_copy(out=sin_cos_s[:], in_=s_turned[:, 0:2 * P:P])
                quantize_x()
            v_between = ROPE_STRIPS <= v_done < N_STRIPS and 0 <= scaled < ROPE_STRIPS <= biased
            if 0 <= scaled < ROPE_STRIPS:
                scale_p(scaled)
            if 0 <= biased < ROPE_STRIPS:
                add_bias_transposed(biased)
            if v_between:
                add_bias_v(v_done)
            if 0 <= scaled < ROPE_STRIPS:
                add_scaled_q(scaled)
            if ROPE_STRIPS <= v_done < N_STRIPS and k != N_STRIPS - 1 and not v_between:
                add_bias_v(v_done)
            if k % 2 == 0 and k // 2 + 1 < N_UNITS:
                for plane in vector_planes(k // 2 + 1):
                    widen(k // 2 + 1, plane, True)
            if k + 1 in EARLY_COPIES:
                interleave(k + 1, "vector")
            if k < N_STRIPS:
                quantize(k)
            if k == N_STRIPS - 1:
                add_bias_v(v_done)

            if k % 4 == 0 and k // 4 + 3 < N_LOADS:
                for g in range(PASSES):
                    new_byte_tile(k // 4 + 3, g)
                    load_bytes(k // 4 + 3, g, 0, LOAD_COLS)

            if 0 <= biased < ROPE_STRIPS:
                rotate_by_d(biased)
            if k == 1:
                mx_matmuls(0)
            if 1 <= k < N_STRIPS:
                mx_matmuls(k)
            if k in IDLE_PASSES:
                keep_clock_up(k, IDLE_PASSES[k])
